import numpy as np
import ml_dtypes


def mxq(x, axis, fmt="e4m3"):
    dtype, down = {"e4m3": (ml_dtypes.float8_e4m3fn, 7), "e5m2": (ml_dtypes.float8_e5m2, 14)}[fmt]
    v = np.moveaxis(np.asarray(x, np.float32).astype(ml_dtypes.bfloat16).astype(np.float64), axis, -1)
    blocks = v.reshape(v.shape[:-1] + (-1, 32))
    amax = np.abs(blocks).max(-1, keepdims=True)
    byte = np.maximum(np.where(amax > 0, np.frexp(amax)[1] - 1 + 127, 0) - down, 1)
    scale = np.exp2(byte - 127.0)
    codes = (blocks / scale).astype(np.float32).astype(dtype).astype(np.float64)
    return np.moveaxis((codes * scale).reshape(v.shape), -1, axis)


WIDE = False


def mx_kscale(k):
    if not WIDE:
        return np.ones(k)
    levels = np.array([10, -10, 5, -5, 0])
    a = np.random.permutation(np.resize(levels, k // 512 * 4)).reshape(k // 512, 4)
    idx = np.arange(k)
    return np.exp2(a[idx // 512, idx % 128 // 32])


BF16 = ml_dtypes.bfloat16


def bf(x):
    return np.asarray(x, np.float32).astype(BF16)


def f64(x):
    return np.asarray(x).astype(np.float64)


B, CL, CH, CK, CV, CO, H, W = 2, 1024, 2048, 256, 512, 1024, 48, 72
N = H * W
PSP = (1, 3, 6, 8)
EPS = 1e-5


def psp(x):
    b, c, h, w = x.shape
    return np.concatenate(
        [x.reshape(b, c, s, h // s, s, w // s).mean(axis=(3, 5)).reshape(b, c, s * s) for s in PSP], axis=2)


def setup_inputs():
    s = mx_kscale(CL)
    return {"low_feats": bf(np.random.standard_normal((B, CL, H, W)) * s[None, :, None, None]),
            "wk": bf(np.random.standard_normal((CK, CL)) * 2.5 / np.sqrt(CL) / s[None, :]),
            "bk": bf(np.random.standard_normal(CK) * 0.3),
            "gk": bf(np.random.uniform(0.5, 1.5, CK)),
            "bek": bf(np.random.standard_normal(CK) * 0.3),
            "mk": bf(np.random.standard_normal(CK) * 0.3),
            "vk": bf(np.random.uniform(0.5, 1.5, CK)),
            "wv": bf(np.random.standard_normal((CV, CL)) * 3.0 / np.sqrt(CL) / s[None, :]),
            "bv": bf(np.random.standard_normal(CV) * 0.3)}


def reference(low_feats, wk, bk, gk, bek, mk, vk, wv, bv):
    xq = mxq(f64(low_feats).reshape(B, CL, N), 1, "e4m3")
    v = (mxq(f64(wv), 1, "e4m3") @ xq) + f64(bv)[None, :, None]
    value = psp(v.reshape(B, CV, H, W)).transpose(0, 2, 1)
    u = (mxq(f64(wk), 1, "e4m3") @ xq) + f64(bk)[None, :, None]
    sc = f64(gk) / np.sqrt(f64(vk) + EPS)
    r = np.maximum((u - f64(mk)[None, :, None]) * sc[None, :, None] + f64(bek)[None, :, None], 0.0)
    key = psp(r.reshape(B, CK, H, W))
    return value, key

@@ -1,0 +1,275 @@
+from contextlib import ExitStack
+
+import concourse.mybir as mybir
+from concourse.masks import make_identity
+
+F32 = mybir.dt.float32
+BF16 = mybir.dt.bfloat16
+U32 = mybir.dt.uint32
+U8 = mybir.dt.uint8
+FP8X4 = mybir.dt.float8_e4m3fn_x4
+ACT = mybir.ActivationFunctionType
+ALU = mybir.AluOpType
+AXIS = mybir.AxisListType
+
+B, CL, CK, CV, H, W = 2, 1024, 256, 512, 48, 72
+GRIDS = (1, 3, 6, 8)
+LOCS = sum(s * s for s in GRIDS)
+EPS = 1e-5
+FLOPS = 2 * (CK + CV) * CL * B * H * W
+
+P = 128
+PACK = 4
+K_PASS = P * PACK
+PASSES = CL // K_PASS
+V_TILES = CV // P
+K_TILES = CK // P
+W_TILES = V_TILES + K_TILES
+
+CELL_H, CELL_W = 2, 3
+PLANES = CELL_H * CELL_W
+CELL_COLS = W // CELL_W
+IMAGE_CELLS = (H // CELL_H) * CELL_COLS
+SLAB_ROWS = 16
+SLAB_CELL_ROWS = SLAB_ROWS // CELL_H
+SLAB_CELLS = SLAB_CELL_ROWS * CELL_COLS
+SLABS_PER_IMAGE = H // SLAB_ROWS
+BLOCK_CELLS = 2 * SLAB_CELLS
+BLOCKS = B * IMAGE_CELLS // BLOCK_CELLS
+CHUNKS = ((0, 128), (128, 256))
+
+
+def tile_afnb_pa_t_kernel(tc, low_feats, wk, bk, gk, bek, mk, vk, wv, bv, out_0, out_1):
+    nc = tc.nc
+    with ExitStack() as stack:
+        const = stack.enter_context(tc.tile_pool(name="const", bufs=1))
+        raw_pool = stack.enter_context(tc.tile_pool(name="raw", bufs=4))
+        grouped_pool = stack.enter_context(tc.tile_pool(name="grouped", bufs=3))
+        codes_pool = stack.enter_context(tc.tile_pool(name="codes", bufs=2))
+        relu_pool = stack.enter_context(tc.tile_pool(name="relu", bufs=6))
+        sum_pool = stack.enter_context(tc.tile_pool(name="sum", bufs=4))
+        out_pool = stack.enter_context(tc.tile_pool(name="out", bufs=2))
+        psum_v = stack.enter_context(tc.psum_pool(name="psum_v", bufs=2))
+        psum_k = stack.enter_context(tc.psum_pool(name="psum_k", bufs=4))
+        psum_t = stack.enter_context(tc.psum_pool(name="psum_t", bufs=2))
+
+        ident = const.tile([P, P], F32)
+        make_identity(nc, ident[:])
+
+        w_codes = const.tile([P, W_TILES, PASSES, P], U32, align_bytes=64)
+        w_scales = const.tile([P, W_TILES, PASSES, P], U8, align_bytes=64)
+        w_grouped = grouped_pool.tile([P, W_TILES, PASSES, P, PACK], BF16, tag="grouped", align_bytes=64)
+        w_grouped_words = w_grouped[:].bitcast(F32)
+        for w_dram, first, count in ((wv, 0, V_TILES), (wk, V_TILES, K_TILES)):
+            w_raw = raw_pool.tile([P, count, CL], BF16, tag="raw")
+            nc.sync.dma_start(out=w_raw[:], in_=w_dram.rearrange("(m p) k -> p m k", p=P))
+            words = w_raw[:].bitcast(F32).rearrange("p m (c q u) -> p m c u q", c=PASSES, q=P, u=2)
+            for i in range(count):
+                m = first + i
+                flipped = psum_t.tile([P, PASSES, 2, P], F32, tag="flip")
+                for c in range(PASSES):
+                    for u in range(2):
+                        nc.tensor.transpose(out=flipped[:, c, u, :], in_=words[:, i, c, u, :], identity=ident[:])
+                copy = nc.vector.tensor_copy if m % 2 == 0 else nc.scalar.copy
+                copy(out=w_grouped_words[:, m], in_=flipped[:].rearrange("p c u r -> p c r u"))
+                nc.vector.quantize_mx(
+                    out=w_codes[:, m].rearrange("p c r -> p (c r)").bitcast(FP8X4),
+                    scales=w_scales[:, m].rearrange("p c r -> p (c r)"),
+                    in_=w_grouped[:, m].rearrange("p c r t -> p (c r t)"),
+                )
+
+        vector_rows = const.tile([P, P], BF16)
+        nc.vector.memset(vector_rows[:], 0.0)
+        row = 0
+        first_row = {}
+        for name, vector in (("bk", bk), ("gk", gk), ("bek", bek), ("mk", mk), ("vk", vk), ("bv", bv)):
+            rows = vector.shape[0] // P
+            nc.scalar.dma_start(out=vector_rows[row : row + rows, :], in_=vector.rearrange("(r c) -> r c", c=P))
+            first_row[name] = row
+            row += rows
+        vector_rows_f32 = const.tile([P, P], F32)
+        nc.vector.tensor_copy(out=vector_rows_f32[:], in_=vector_rows[:])
+        vector_flipped = psum_t.tile([P, P], F32, tag="flip")
+        nc.tensor.transpose(out=vector_flipped[:], in_=vector_rows_f32[:], identity=ident[:])
+        columns = const.tile([P, row], F32)
+        nc.vector.tensor_copy(out=columns[:], in_=vector_flipped[:, 0:row])
+
+        def column(name, count):
+            return columns[:, first_row[name] : first_row[name] + count]
+
+        var_eps = const.tile([P, K_TILES], F32)
+        nc.vector.tensor_scalar_add(out=var_eps[:], in0=column("vk", K_TILES), scalar1=EPS)
+        std = const.tile([P, K_TILES], F32)
+        nc.scalar.activation(out=std[:], in_=var_eps[:], func=ACT.Sqrt)
+        inv_std = const.tile([P, K_TILES], F32)
+        nc.vector.reciprocal(out=inv_std[:], in_=std[:])
+        bn_scale = const.tile([P, K_TILES], F32)
+        nc.vector.tensor_mul(out=bn_scale[:], in0=column("gk", K_TILES), in1=inv_std[:])
+        centred = const.tile([P, K_TILES], F32)
+        nc.vector.tensor_sub(out=centred[:], in0=column("bk", K_TILES), in1=column("mk", K_TILES))
+        scaled = const.tile([P, K_TILES], F32)
+        nc.vector.tensor_mul(out=scaled[:], in0=centred[:], in1=bn_scale[:])
+        bn_shift = const.tile([P, K_TILES], F32)
+        nc.vector.tensor_add(out=bn_shift[:], in0=scaled[:], in1=column("bek", K_TILES))
+        cell_bias = const.tile([P, V_TILES], F32)
+        nc.vector.tensor_scalar_mul(out=cell_bias[:], in0=column("bv", V_TILES), scalar1=float(PLANES))
+
+        area_row = const.tile([P, P], F32)
+        nc.vector.memset(area_row[:], 1.0)
+        level_first = {}
+        first = 0
+        for s in GRIDS:
+            nc.vector.memset(area_row[:, first : first + s * s], float((H // s) * (W // s)))
+            level_first[s] = first
+            first += s * s
+        inv_area_row = const.tile([P, P], F32)
+        nc.vector.reciprocal(out=inv_area_row[:], in_=area_row[:])
+        area_flipped = psum_t.tile([P, P], F32, tag="flip")
+        nc.tensor.transpose(out=area_flipped[:], in_=inv_area_row[:], identity=ident[:])
+        inv_area_col = const.tile([P, 1], F32)
+        nc.vector.tensor_copy(out=inv_area_col[:], in_=area_flipped[:, 0:1])
+
+        cells = const.tile([P, W_TILES, B * IMAGE_CELLS], F32)
+        value_sums = const.tile([P, V_TILES, B, P], F32)
+        nc.vector.memset(value_sums[:, :, :, LOCS:], 0.0)
+        key_sums = const.tile([P, K_TILES, B, LOCS], F32)
+
+        def level(sums, s):
+            return sums[:, level_first[s] : level_first[s] + s * s]
+
+        def grid_sums(out, in_, s, side):
+            nc.vector.tensor_reduce(
+                out=out.rearrange("p (a c) -> p a c", a=s),
+                in_=in_.rearrange("p (a i c k) -> p a c i k", a=s, i=side // s, c=s, k=side // s),
+                axis=AXIS.XY,
+                op=ALU.add,
+            )
+
+        def pool_image(image_cells, sums):
+            grid_sums(level(sums, 8), image_cells, 8, CELL_COLS)
+            grid_sums(level(sums, 6), image_cells, 6, CELL_COLS)
+            grid_sums(level(sums, 3), level(sums, 6), 3, 6)
+            grid_sums(level(sums, 1), level(sums, 3), 1, 3)
+
+        def load_slab(slab, c):
+            b, part = divmod(slab, SLABS_PER_IMAGE)
+            raw = raw_pool.tile([P, PACK, SLAB_ROWS * W], BF16, tag="raw")
+            rows = low_feats[b, c * K_PASS : (c + 1) * K_PASS, part * SLAB_ROWS : (part + 1) * SLAB_ROWS, :]
+            nc.sync.dma_start(out=raw[:], in_=rows.rearrange("(p t) h w -> p t (h w)", t=PACK))
+            return raw
+
+        def regroup(raw, grouped, half):
+            src = raw[:].rearrange(
+                "p t (hi jh cw jw) -> p jh jw hi cw t", hi=SLAB_CELL_ROWS, jh=CELL_H, cw=CELL_COLS, jw=CELL_W
+            )
+            dst = grouped[:, :, half * SLAB_CELLS : (half + 1) * SLAB_CELLS, :].rearrange(
+                "p (jh jw) (hi cw) t -> p jh jw hi cw t", jh=CELL_H, jw=CELL_W, hi=SLAB_CELL_ROWS, cw=CELL_COLS
+            )
+            nc.vector.tensor_copy(out=dst[:, 0], in_=src[:, 0])
+            for jw in range(CELL_W):
+                nc.scalar.copy(out=dst[:, 1, jw], in_=src[:, 1, jw])
+
+        def mx_pass(acc, m, c, j, codes, scales, cols, start, stop):
+            nc.tensor.matmul_mx(
+                out=acc,
+                lhsT=w_codes[:, m, c, :].bitcast(FP8X4),
+                lhsT_scale=w_scales[:, m, c, :],
+                rhs=codes[:, c, j, cols].bitcast(FP8X4),
+                rhs_scale=scales[:, c, j, cols],
+                start=start,
+                stop=stop,
+            )
+
+        def store_value(b):
+            flipped = psum_t.tile([P, V_TILES, P], F32, tag="flip")
+            for m in range(V_TILES):
+                nc.tensor.transpose(out=flipped[:, m, :], in_=value_sums[:, m, b, :], identity=ident[:])
+            value_rows = out_pool.tile([P, CV], F32)
+            nc.scalar.activation(
+                out=value_rows[:],
+                in_=flipped[:].rearrange("p m r -> p (m r)"),
+                func=ACT.Copy,
+                scale=inv_area_col[:, 0:1],
+            )
+            nc.sync.dma_start(out=out_0[b], in_=value_rows[0:LOCS, :])
+
+        def store_key(b, mk_tile):
+            key_rows = out_pool.tile([P, LOCS], F32)
+            nc.vector.tensor_mul(out=key_rows[:], in0=key_sums[:, mk_tile, b, :], in1=inv_area_row[:, 0:LOCS])
+            nc.sync.dma_start(out=out_1[b, mk_tile * P : (mk_tile + 1) * P, :], in_=key_rows[:])
+
+        def compute_chunk(codes, scales, block, lo, n):
+            cols = slice(lo, lo + n)
+            first_cell = block * BLOCK_CELLS + lo
+            out_cells = slice(first_cell, first_cell + n)
+            done = [b for b in range(B) if first_cell < (b + 1) * IMAGE_CELLS <= first_cell + n]
+
+            def image_cells(m, b):
+                return cells[:, m, b * IMAGE_CELLS : (b + 1) * IMAGE_CELLS]
+
+            for pair in range(V_TILES // 2):
+                acc_v = psum_v.tile([P, 2, n], F32, tag="acc_v")
+                for i in range(2):
+                    m = 2 * pair + i
+                    for c in range(PASSES):
+                        for j in range(PLANES):
+                            mx_pass(
+                                acc_v[:, i, :], m, c, j, codes, scales, cols,
+                                start=(c == 0 and j == 0), stop=(c == PASSES - 1 and j == PLANES - 1),
+                            )
+                for i in range(2):
+                    m = 2 * pair + i
+                    nc.scalar.activation(
+                        out=cells[:, m, out_cells], in_=acc_v[:, i, :], func=ACT.Identity,
+                        bias=cell_bias[:, m : m + 1], scale=1.0,
+                    )
+                    for b in done:
+                        pool_image(image_cells(m, b), value_sums[:, m, b, :])
+            for b in done:
+                store_value(b)
+
+            for mk_tile in range(K_TILES):
+                m = V_TILES + mk_tile
+                total = None
+                for pair in range(PLANES // 2):
+                    acc_k = psum_k.tile([P, 2, n], F32, tag="acc_k")
+                    for i in range(2):
+                        for c in range(PASSES):
+                            mx_pass(
+                                acc_k[:, i, :], m, c, 2 * pair + i, codes, scales, cols,
+                                start=(c == 0), stop=(c == PASSES - 1),
+                            )
+                    relu = relu_pool.tile([P, 2, n], F32, tag="relu")
+                    nc.scalar.activation(
+                        out=relu[:], in_=acc_k[:], func=ACT.Relu,
+                        bias=bn_shift[:, mk_tile : mk_tile + 1], scale=bn_scale[:, mk_tile : mk_tile + 1],
+                    )
+                    if total is None:
+                        total = relu
+                    else:
+                        longer = sum_pool.tile([P, 2, n], F32, tag="sum")
+                        nc.vector.tensor_add(out=longer[:], in0=total[:], in1=relu[:])
+                        total = longer
+                nc.vector.tensor_add(out=cells[:, m, out_cells], in0=total[:, 0, :], in1=total[:, 1, :])
+                for b in done:
+                    pool_image(image_cells(m, b), key_sums[:, mk_tile, b, :])
+                    store_key(b, mk_tile)
+
+        for block in range(BLOCKS):
+            codes = codes_pool.tile([P, PASSES, PLANES, BLOCK_CELLS], U32, tag="codes", align_bytes=64)
+            scales = codes_pool.tile([P, PASSES, PLANES, BLOCK_CELLS], U8, tag="scales", align_bytes=64)
+            grouped = []
+            for c in range(PASSES):
+                grouped_c = grouped_pool.tile([P, PLANES, BLOCK_CELLS, PACK], BF16, tag="grouped", align_bytes=64)
+                grouped.append(grouped_c)
+            for half, (lo, n) in enumerate(CHUNKS):
+                for c in range(PASSES):
+                    regroup(load_slab(2 * block + half, c), grouped[c], half)
+                for c in range(PASSES):
+                    for j in range(PLANES):
+                        nc.vector.quantize_mx(
+                            out=codes[:, c, j, lo : lo + n].bitcast(FP8X4),
+                            scales=scales[:, c, j, lo : lo + n],
+                            in_=grouped[c][:, j, lo : lo + n, :].rearrange("p w t -> p (w t)"),
+                        )
+                compute_chunk(codes, scales, block, lo, n)

@@ -160,14 +160,14 @@ def tile_afnb_pa_t_kernel(tc, low_feats, wk, bk, gk, bek, mk, vk, wv, bv, out_0,
 
         def regroup(raw, grouped, half):
             src = raw[:].rearrange(
-                "p t (hi jh cw jw) -> p jh jw hi cw t", hi=SLAB_CELL_ROWS, jh=CELL_H, cw=CELL_COLS, jw=CELL_W
+                "p t (hi jh cw jw) -> p jh hi jw cw t", hi=SLAB_CELL_ROWS, jh=CELL_H, cw=CELL_COLS, jw=CELL_W
             )
             dst = grouped[:, :, half * SLAB_CELLS : (half + 1) * SLAB_CELLS, :].rearrange(
-                "p (jh jw) (hi cw) t -> p jh jw hi cw t", jh=CELL_H, jw=CELL_W, hi=SLAB_CELL_ROWS, cw=CELL_COLS
+                "p (jh jw) (hi cw) t -> p jh hi jw cw t", jh=CELL_H, jw=CELL_W, hi=SLAB_CELL_ROWS, cw=CELL_COLS
             )
             nc.vector.tensor_copy(out=dst[:, 0], in_=src[:, 0])
             for jw in range(CELL_W):
-                nc.scalar.copy(out=dst[:, 1, jw], in_=src[:, 1, jw])
+                nc.scalar.copy(out=dst[:, 1, :, jw], in_=src[:, 1, :, jw])
 
         def mx_pass(acc, m, c, j, codes, scales, cols, start, stop):
             nc.tensor.matmul_mx(

@@ -166,7 +166,8 @@ def tile_afnb_pa_t_kernel(tc, low_feats, wk, bk, gk, bek, mk, vk, wv, bv, out_0,
                 "p (jh jw) (hi cw) t -> p jh hi jw cw t", jh=CELL_H, jw=CELL_W, hi=SLAB_CELL_ROWS, cw=CELL_COLS
             )
             nc.vector.tensor_copy(out=dst[:, 0], in_=src[:, 0])
-            for jw in range(CELL_W):
+            nc.vector.tensor_copy(out=dst[:, 1, :, 0], in_=src[:, 1, :, 0])
+            for jw in range(1, CELL_W):
                 nc.scalar.copy(out=dst[:, 1, :, jw], in_=src[:, 1, :, jw])
 
         def mx_pass(acc, m, c, j, codes, scales, cols, start, stop):

@@ -160,15 +160,15 @@ def tile_afnb_pa_t_kernel(tc, low_feats, wk, bk, gk, bek, mk, vk, wv, bv, out_0,
 
         def regroup(raw, grouped, half):
             src = raw[:].rearrange(
-                "p t (hi jh cw jw) -> p jh hi jw cw t", hi=SLAB_CELL_ROWS, jh=CELL_H, cw=CELL_COLS, jw=CELL_W
+                "p t (hi jh cp i jw) -> p jh hi cp t i jw",
+                hi=SLAB_CELL_ROWS, jh=CELL_H, cp=CELL_COLS // 2, i=2, jw=CELL_W,
             )
             dst = grouped[:, :, half * SLAB_CELLS : (half + 1) * SLAB_CELLS, :].rearrange(
-                "p (jh jw) (hi cw) t -> p jh hi jw cw t", jh=CELL_H, jw=CELL_W, hi=SLAB_CELL_ROWS, cw=CELL_COLS
+                "p (jh jw) (hi cp i) t -> p jh hi cp t i jw",
+                jh=CELL_H, jw=CELL_W, hi=SLAB_CELL_ROWS, cp=CELL_COLS // 2, i=2,
             )
             nc.vector.tensor_copy(out=dst[:, 0], in_=src[:, 0])
-            nc.vector.tensor_copy(out=dst[:, 1, :, 0], in_=src[:, 1, :, 0])
-            for jw in range(1, CELL_W):
-                nc.scalar.copy(out=dst[:, 1, :, jw], in_=src[:, 1, :, jw])
+            nc.scalar.copy(out=dst[:, 1], in_=src[:, 1])
 
         def mx_pass(acc, m, c, j, codes, scales, cols, start, stop):
             nc.tensor.matmul_mx(

@@ -37,46 +37,33 @@ SLABS_PER_IMAGE = H // SLAB_ROWS
 BLOCK_CELLS = 2 * SLAB_CELLS
 BLOCKS = B * IMAGE_CELLS // BLOCK_CELLS
 CHUNKS = ((0, 128), (128, 256))
+SLABS = B * SLABS_PER_IMAGE
+AHEAD = 2
+RELU_BUFS = 9
 
 
 def tile_afnb_pa_t_kernel(tc, low_feats, wk, bk, gk, bek, mk, vk, wv, bv, out_0, out_1):
     nc = tc.nc
     with ExitStack() as stack:
         const = stack.enter_context(tc.tile_pool(name="const", bufs=1))
-        raw_pool = stack.enter_context(tc.tile_pool(name="raw", bufs=4))
-        grouped_pool = stack.enter_context(tc.tile_pool(name="grouped", bufs=3))
+        raw_pool = stack.enter_context(tc.tile_pool(name="raw", bufs=2 * PASSES))
+        grouped_pool = stack.enter_context(tc.tile_pool(name="grouped", bufs=2 * PASSES))
         codes_pool = stack.enter_context(tc.tile_pool(name="codes", bufs=2))
-        relu_pool = stack.enter_context(tc.tile_pool(name="relu", bufs=6))
-        sum_pool = stack.enter_context(tc.tile_pool(name="sum", bufs=4))
+        relu_pool = stack.enter_context(tc.tile_pool(name="relu", bufs=RELU_BUFS))
         out_pool = stack.enter_context(tc.tile_pool(name="out", bufs=2))
         psum_v = stack.enter_context(tc.psum_pool(name="psum_v", bufs=2))
-        psum_k = stack.enter_context(tc.psum_pool(name="psum_k", bufs=4))
-        psum_t = stack.enter_context(tc.psum_pool(name="psum_t", bufs=2))
+        psum_k = stack.enter_context(tc.psum_pool(name="psum_k", bufs=6))
 
-        ident = const.tile([P, P], F32)
-        make_identity(nc, ident[:])
+        raws = {}
 
-        w_codes = const.tile([P, W_TILES, PASSES, P], U32, align_bytes=64)
-        w_scales = const.tile([P, W_TILES, PASSES, P], U8, align_bytes=64)
-        w_grouped = grouped_pool.tile([P, W_TILES, PASSES, P, PACK], BF16, tag="grouped", align_bytes=64)
-        w_grouped_words = w_grouped[:].bitcast(F32)
-        for w_dram, first, count in ((wv, 0, V_TILES), (wk, V_TILES, K_TILES)):
-            w_raw = raw_pool.tile([P, count, CL], BF16, tag="raw")
-            nc.sync.dma_start(out=w_raw[:], in_=w_dram.rearrange("(m p) k -> p m k", p=P))
-            words = w_raw[:].bitcast(F32).rearrange("p m (c q u) -> p m c u q", c=PASSES, q=P, u=2)
-            for i in range(count):
-                m = first + i
-                flipped = psum_t.tile([P, PASSES, 2, P], F32, tag="flip")
-                for c in range(PASSES):
-                    for u in range(2):
-                        nc.tensor.transpose(out=flipped[:, c, u, :], in_=words[:, i, c, u, :], identity=ident[:])
-                copy = nc.vector.tensor_copy if m % 2 == 0 else nc.scalar.copy
-                copy(out=w_grouped_words[:, m], in_=flipped[:].rearrange("p c u r -> p c r u"))
-                nc.vector.quantize_mx(
-                    out=w_codes[:, m].rearrange("p c r -> p (c r)").bitcast(FP8X4),
-                    scales=w_scales[:, m].rearrange("p c r -> p (c r)"),
-                    in_=w_grouped[:, m].rearrange("p c r t -> p (c r t)"),
-                )
+        def load_slab(slab):
+            b, part = divmod(slab, SLABS_PER_IMAGE)
+            raws[slab] = []
+            for c in range(PASSES):
+                raw = raw_pool.tile([P, PACK, SLAB_ROWS * W], BF16, tag="raw")
+                rows = low_feats[b, c * K_PASS : (c + 1) * K_PASS, part * SLAB_ROWS : (part + 1) * SLAB_ROWS, :]
+                nc.sync.dma_start(out=raw[:], in_=rows.rearrange("(p t) h w -> p t (h w)", t=PACK))
+                raws[slab].append(raw)
 
         vector_rows = const.tile([P, P], BF16)
         nc.vector.memset(vector_rows[:], 0.0)
@@ -87,32 +74,15 @@ def tile_afnb_pa_t_kernel(tc, low_feats, wk, bk, gk, bek, mk, vk, wv, bv, out_0,
             nc.scalar.dma_start(out=vector_rows[row : row + rows, :], in_=vector.rearrange("(r c) -> r c", c=P))
             first_row[name] = row
             row += rows
-        vector_rows_f32 = const.tile([P, P], F32)
-        nc.vector.tensor_copy(out=vector_rows_f32[:], in_=vector_rows[:])
-        vector_flipped = psum_t.tile([P, P], F32, tag="flip")
-        nc.tensor.transpose(out=vector_flipped[:], in_=vector_rows_f32[:], identity=ident[:])
-        columns = const.tile([P, row], F32)
-        nc.vector.tensor_copy(out=columns[:], in_=vector_flipped[:, 0:row])
+        load_slab(0)
+        w_raws = []
+        for w_dram, count in ((wv, V_TILES), (wk, K_TILES)):
+            w_raw = raw_pool.tile([P, count, CL], BF16, tag="raw")
+            nc.sync.dma_start(out=w_raw[:], in_=w_dram.rearrange("(m p) k -> p m k", p=P))
+            w_raws.append(w_raw)
 
-        def column(name, count):
-            return columns[:, first_row[name] : first_row[name] + count]
-
-        var_eps = const.tile([P, K_TILES], F32)
-        nc.vector.tensor_scalar_add(out=var_eps[:], in0=column("vk", K_TILES), scalar1=EPS)
-        std = const.tile([P, K_TILES], F32)
-        nc.scalar.activation(out=std[:], in_=var_eps[:], func=ACT.Sqrt)
-        inv_std = const.tile([P, K_TILES], F32)
-        nc.vector.reciprocal(out=inv_std[:], in_=std[:])
-        bn_scale = const.tile([P, K_TILES], F32)
-        nc.vector.tensor_mul(out=bn_scale[:], in0=column("gk", K_TILES), in1=inv_std[:])
-        centred = const.tile([P, K_TILES], F32)
-        nc.vector.tensor_sub(out=centred[:], in0=column("bk", K_TILES), in1=column("mk", K_TILES))
-        scaled = const.tile([P, K_TILES], F32)
-        nc.vector.tensor_mul(out=scaled[:], in0=centred[:], in1=bn_scale[:])
-        bn_shift = const.tile([P, K_TILES], F32)
-        nc.vector.tensor_add(out=bn_shift[:], in0=scaled[:], in1=column("bek", K_TILES))
-        cell_bias = const.tile([P, V_TILES], F32)
-        nc.vector.tensor_scalar_mul(out=cell_bias[:], in0=column("bv", V_TILES), scalar1=float(PLANES))
+        ident = const.tile([P, P], F32)
+        make_identity(nc, ident[:])
 
         area_row = const.tile([P, P], F32)
         nc.vector.memset(area_row[:], 1.0)
@@ -124,39 +94,69 @@ def tile_afnb_pa_t_kernel(tc, low_feats, wk, bk, gk, bek, mk, vk, wv, bv, out_0,
             first += s * s
         inv_area_row = const.tile([P, P], F32)
         nc.vector.reciprocal(out=inv_area_row[:], in_=area_row[:])
-        area_flipped = psum_t.tile([P, P], F32, tag="flip")
+        area_flipped = psum_k.tile([P, P], F32, tag="acc_k")
         nc.tensor.transpose(out=area_flipped[:], in_=inv_area_row[:], identity=ident[:])
         inv_area_col = const.tile([P, 1], F32)
         nc.vector.tensor_copy(out=inv_area_col[:], in_=area_flipped[:, 0:1])
+
+        vector_rows_f32 = const.tile([P, P], F32)
+        nc.vector.tensor_copy(out=vector_rows_f32[:], in_=vector_rows[:])
+        vector_flipped = psum_k.tile([P, P], F32, tag="acc_k")
+        nc.tensor.transpose(out=vector_flipped[:], in_=vector_rows_f32[:], identity=ident[:])
+        columns = const.tile([P, row], F32)
+        nc.vector.tensor_copy(out=columns[:], in_=vector_flipped[:, 0:row])
+
+        def column(name, count):
+            return columns[:, first_row[name] : first_row[name] + count]
+
+        var_eps = const.tile([P, K_TILES], F32)
+        nc.vector.tensor_scalar_add(out=var_eps[:], in0=column("vk", K_TILES), scalar1=EPS)
+        std = const.tile([P, K_TILES], F32)
+        nc.scalar.activation(out=std[:], in_=var_eps[:], func=ACT.Sqrt)
+        centred = const.tile([P, K_TILES], F32)
+        nc.vector.tensor_sub(out=centred[:], in0=column("bk", K_TILES), in1=column("mk", K_TILES))
+        bias_area = const.tile([P, V_TILES, P], F32)
+        for m in range(V_TILES):
+            nc.vector.tensor_scalar_mul(
+                out=bias_area[:, m, :], in0=area_row[:], scalar1=column("bv", V_TILES)[:, m : m + 1]
+            )
+        inv_std = const.tile([P, K_TILES], F32)
+        nc.vector.reciprocal(out=inv_std[:], in_=std[:])
+        bn_scale = const.tile([P, K_TILES], F32)
+        nc.vector.tensor_mul(out=bn_scale[:], in0=column("gk", K_TILES), in1=inv_std[:])
+        scaled = const.tile([P, K_TILES], F32)
+        nc.vector.tensor_mul(out=scaled[:], in0=centred[:], in1=bn_scale[:])
+        bn_shift = const.tile([P, K_TILES], F32)
+        nc.vector.tensor_add(out=bn_shift[:], in0=scaled[:], in1=column("bek", K_TILES))
 
         cells = const.tile([P, W_TILES, B * IMAGE_CELLS], F32)
         value_sums = const.tile([P, V_TILES, B, P], F32)
         nc.vector.memset(value_sums[:, :, :, LOCS:], 0.0)
         key_sums = const.tile([P, K_TILES, B, LOCS], F32)
 
-        def level(sums, s):
-            return sums[:, level_first[s] : level_first[s] + s * s]
+        w_codes = const.tile([P, W_TILES, PASSES, P], U32, align_bytes=64)
+        w_scales = const.tile([P, W_TILES, PASSES, P], U8, align_bytes=64)
 
-        def grid_sums(out, in_, s, side):
-            nc.vector.tensor_reduce(
-                out=out.rearrange("p (a c) -> p a c", a=s),
-                in_=in_.rearrange("p (a i c k) -> p a c i k", a=s, i=side // s, c=s, k=side // s),
-                axis=AXIS.XY,
-                op=ALU.add,
-            )
-
-        def pool_image(image_cells, sums):
-            grid_sums(level(sums, 8), image_cells, 8, CELL_COLS)
-            grid_sums(level(sums, 6), image_cells, 6, CELL_COLS)
-            grid_sums(level(sums, 3), level(sums, 6), 3, 6)
-            grid_sums(level(sums, 1), level(sums, 3), 1, 3)
-
-        def load_slab(slab, c):
-            b, part = divmod(slab, SLABS_PER_IMAGE)
-            raw = raw_pool.tile([P, PACK, SLAB_ROWS * W], BF16, tag="raw")
-            rows = low_feats[b, c * K_PASS : (c + 1) * K_PASS, part * SLAB_ROWS : (part + 1) * SLAB_ROWS, :]
-            nc.sync.dma_start(out=raw[:], in_=rows.rearrange("(p t) h w -> p t (h w)", t=PACK))
-            return raw
+        def quantise_weights():
+            w_grouped = grouped_pool.tile([P, W_TILES, PASSES, P, PACK], BF16, tag="grouped", align_bytes=64)
+            w_grouped_words = w_grouped[:].bitcast(F32)
+            m = 0
+            for w_raw, count in zip(w_raws, (V_TILES, K_TILES)):
+                words = w_raw[:].bitcast(F32).rearrange("p m (c q u) -> p m c u q", c=PASSES, q=P, u=2)
+                for i in range(count):
+                    flipped = psum_k.tile([P, PASSES, 2, P], F32, tag="acc_k")
+                    for c in range(PASSES):
+                        for u in range(2):
+                            nc.tensor.transpose(out=flipped[:, c, u, :], in_=words[:, i, c, u, :], identity=ident[:])
+                    copy = nc.vector.tensor_copy if m % 2 == 0 else nc.scalar.copy
+                    copy(out=w_grouped_words[:, m], in_=flipped[:].rearrange("p c u r -> p c r u"))
+                    m += 1
+            for m in range(W_TILES):
+                nc.vector.quantize_mx(
+                    out=w_codes[:, m].rearrange("p c r -> p (c r)").bitcast(FP8X4),
+                    scales=w_scales[:, m].rearrange("p c r -> p (c r)"),
+                    in_=w_grouped[:, m].rearrange("p c r t -> p (c r t)"),
+                )
 
         def regroup(raw, grouped, half):
             src = raw[:].rearrange(
@@ -170,22 +170,125 @@ def tile_afnb_pa_t_kernel(tc, low_feats, wk, bk, gk, bek, mk, vk, wv, bv, out_0,
             nc.vector.tensor_copy(out=dst[:, 0], in_=src[:, 0])
             nc.scalar.copy(out=dst[:, 1], in_=src[:, 1])
 
-        def mx_pass(acc, m, c, j, codes, scales, cols, start, stop):
-            nc.tensor.matmul_mx(
-                out=acc,
-                lhsT=w_codes[:, m, c, :].bitcast(FP8X4),
-                lhsT_scale=w_scales[:, m, c, :],
-                rhs=codes[:, c, j, cols].bitcast(FP8X4),
-                rhs_scale=scales[:, c, j, cols],
-                start=start,
-                stop=stop,
+        blocks = {}
+
+        def feed(slab):
+            block, half = divmod(slab, 2)
+            if half == 0:
+                codes = codes_pool.tile([P, PASSES, PLANES, BLOCK_CELLS], U32, tag="codes", align_bytes=64)
+                scales = codes_pool.tile([P, PASSES, PLANES, BLOCK_CELLS], U8, tag="scales", align_bytes=64)
+                grouped = []
+                for c in range(PASSES):
+                    grouped_c = grouped_pool.tile([P, PLANES, BLOCK_CELLS, PACK], BF16, tag="grouped", align_bytes=64)
+                    grouped.append(grouped_c)
+                blocks[block] = (grouped, codes, scales)
+            grouped, codes, scales = blocks[block]
+            for c in range(PASSES):
+                regroup(raws[slab][c], grouped[c], half)
+            lo, n = CHUNKS[half]
+            for c in range(PASSES):
+                for j in range(PLANES):
+                    nc.vector.quantize_mx(
+                        out=codes[:, c, j, lo : lo + n].bitcast(FP8X4),
+                        scales=scales[:, c, j, lo : lo + n],
+                        in_=grouped[c][:, j, lo : lo + n, :].rearrange("p w t -> p (w t)"),
+                    )
+
+        def multiply(chunk):
+            block, half = divmod(chunk, 2)
+            grouped, codes, scales = blocks[block]
+            lo, n = CHUNKS[half]
+            first_cell = block * BLOCK_CELLS + lo
+
+            def mx_pass(acc, m, c, j, start, stop):
+                nc.tensor.matmul_mx(
+                    out=acc,
+                    lhsT=w_codes[:, m, c, :].bitcast(FP8X4),
+                    lhsT_scale=w_scales[:, m, c, :],
+                    rhs=codes[:, c, j, lo : lo + n].bitcast(FP8X4),
+                    rhs_scale=scales[:, c, j, lo : lo + n],
+                    start=start,
+                    stop=stop,
+                )
+
+            for pair in range(V_TILES // 2):
+                acc_v = psum_v.tile([P, 2, n], F32, tag="acc_v")
+                for i in range(2):
+                    for c in range(PASSES):
+                        for j in range(PLANES):
+                            mx_pass(
+                                acc_v[:, i, :], 2 * pair + i, c, j,
+                                start=(c == 0 and j == 0), stop=(c == PASSES - 1 and j == PLANES - 1),
+                            )
+                nc.scalar.copy(out=cells[:, 2 * pair : 2 * pair + 2, first_cell : first_cell + n], in_=acc_v[:])
+            relus = []
+            for mk_tile in range(K_TILES):
+                relus.append([])
+                for pair in range(PLANES // 2):
+                    acc_k = psum_k.tile([P, 2, n], F32, tag="acc_k")
+                    for i in range(2):
+                        for c in range(PASSES):
+                            mx_pass(
+                                acc_k[:, i, :], V_TILES + mk_tile, c, 2 * pair + i,
+                                start=(c == 0), stop=(c == PASSES - 1),
+                            )
+                    relu = relu_pool.tile([P, 2, n], F32, tag="relu")
+                    nc.scalar.activation(
+                        out=relu[:], in_=acc_k[:], func=ACT.Relu,
+                        bias=bn_shift[:, mk_tile : mk_tile + 1], scale=bn_scale[:, mk_tile : mk_tile + 1],
+                    )
+                    relus[mk_tile].append(relu)
+            return relus
+
+        def add_planes(chunk, relus):
+            block, half = divmod(chunk, 2)
+            lo, n = CHUNKS[half]
+            first_cell = block * BLOCK_CELLS + lo
+            for pair in range(1, PLANES // 2):
+                for planes in relus:
+                    nc.vector.tensor_add(out=planes[0][:], in0=planes[0][:], in1=planes[pair][:])
+            for mk_tile, planes in enumerate(relus):
+                nc.vector.tensor_add(
+                    out=cells[:, V_TILES + mk_tile, first_cell : first_cell + n],
+                    in0=planes[0][:, 0, :], in1=planes[0][:, 1, :],
+                )
+
+        def level(sums, s):
+            return sums[:, level_first[s] : level_first[s] + s * s]
+
+        def grid_sums(out, in_, s, side):
+            nc.vector.tensor_reduce(
+                out=out.rearrange("p (a c) -> p a c", a=s),
+                in_=in_.rearrange("p (a i c k) -> p a c i k", a=s, i=side // s, c=s, k=side // s),
+                axis=AXIS.XY,
+                op=ALU.add,
             )
 
-        def store_value(b):
-            flipped = psum_t.tile([P, V_TILES, P], F32, tag="flip")
+        def pool_image(b, tiles):
+            for s in (8, 6):
+                for m, sums in tiles:
+                    grid_sums(level(sums, s), cells[:, m, b * IMAGE_CELLS : (b + 1) * IMAGE_CELLS], s, CELL_COLS)
+            for m, sums in tiles:
+                grid_sums(level(sums, 3), level(sums, 6), 3, 6)
+            for m, sums in tiles:
+                grid_sums(level(sums, 1), level(sums, 3), 1, 3)
+
+        def pool_values(b):
+            pool_image(b, [(m, value_sums[:, m, b, :]) for m in range(V_TILES)])
+            nc.vector.tensor_add(out=value_sums[:, :, b, :], in0=value_sums[:, :, b, :], in1=bias_area[:])
+
+        def pool_and_store_keys(b):
+            pool_image(b, [(V_TILES + mk_tile, key_sums[:, mk_tile, b, :]) for mk_tile in range(K_TILES)])
+            for mk_tile in range(K_TILES):
+                key_rows = out_pool.tile([P, LOCS], F32, tag="key_rows")
+                nc.vector.tensor_mul(out=key_rows[:], in0=key_sums[:, mk_tile, b, :], in1=inv_area_row[:, 0:LOCS])
+                nc.sync.dma_start(out=out_1[b, mk_tile * P : (mk_tile + 1) * P, :], in_=key_rows[:])
+
+        def store_values(b):
+            flipped = psum_k.tile([P, V_TILES, P], F32, tag="acc_k")
             for m in range(V_TILES):
                 nc.tensor.transpose(out=flipped[:, m, :], in_=value_sums[:, m, b, :], identity=ident[:])
-            value_rows = out_pool.tile([P, CV], F32)
+            value_rows = out_pool.tile([P, CV], F32, tag="value_rows")
             nc.scalar.activation(
                 out=value_rows[:],
                 in_=flipped[:].rearrange("p m r -> p (m r)"),
@@ -194,83 +297,23 @@ def tile_afnb_pa_t_kernel(tc, low_feats, wk, bk, gk, bek, mk, vk, wv, bv, out_0,
             )
             nc.sync.dma_start(out=out_0[b], in_=value_rows[0:LOCS, :])
 
-        def store_key(b, mk_tile):
-            key_rows = out_pool.tile([P, LOCS], F32)
-            nc.vector.tensor_mul(out=key_rows[:], in0=key_sums[:, mk_tile, b, :], in1=inv_area_row[:, 0:LOCS])
-            nc.sync.dma_start(out=out_1[b, mk_tile * P : (mk_tile + 1) * P, :], in_=key_rows[:])
-
-        def compute_chunk(codes, scales, block, lo, n):
-            cols = slice(lo, lo + n)
-            first_cell = block * BLOCK_CELLS + lo
-            out_cells = slice(first_cell, first_cell + n)
-            done = [b for b in range(B) if first_cell < (b + 1) * IMAGE_CELLS <= first_cell + n]
-
-            def image_cells(m, b):
-                return cells[:, m, b * IMAGE_CELLS : (b + 1) * IMAGE_CELLS]
-
-            for pair in range(V_TILES // 2):
-                acc_v = psum_v.tile([P, 2, n], F32, tag="acc_v")
-                for i in range(2):
-                    m = 2 * pair + i
-                    for c in range(PASSES):
-                        for j in range(PLANES):
-                            mx_pass(
-                                acc_v[:, i, :], m, c, j, codes, scales, cols,
-                                start=(c == 0 and j == 0), stop=(c == PASSES - 1 and j == PLANES - 1),
-                            )
-                for i in range(2):
-                    m = 2 * pair + i
-                    nc.scalar.activation(
-                        out=cells[:, m, out_cells], in_=acc_v[:, i, :], func=ACT.Identity,
-                        bias=cell_bias[:, m : m + 1], scale=1.0,
-                    )
-                    for b in done:
-                        pool_image(image_cells(m, b), value_sums[:, m, b, :])
+        feed(0)
+        load_slab(1)
+        quantise_weights()
+        load_slab(2)
+        feed(1)
+        for chunk in range(SLABS):
+            if chunk + AHEAD < SLABS:
+                if chunk + AHEAD + 1 < SLABS:
+                    load_slab(chunk + AHEAD + 1)
+                feed(chunk + AHEAD)
+            relus = multiply(chunk)
+            last_cell = (chunk // 2) * BLOCK_CELLS + sum(CHUNKS[chunk % 2])
+            done = [b for b in range(B) if last_cell - CHUNKS[chunk % 2][1] < (b + 1) * IMAGE_CELLS <= last_cell]
             for b in done:
-                store_value(b)
-
-            for mk_tile in range(K_TILES):
-                m = V_TILES + mk_tile
-                total = None
-                for pair in range(PLANES // 2):
-                    acc_k = psum_k.tile([P, 2, n], F32, tag="acc_k")
-                    for i in range(2):
-                        for c in range(PASSES):
-                            mx_pass(
-                                acc_k[:, i, :], m, c, 2 * pair + i, codes, scales, cols,
-                                start=(c == 0), stop=(c == PASSES - 1),
-                            )
-                    relu = relu_pool.tile([P, 2, n], F32, tag="relu")
-                    nc.scalar.activation(
-                        out=relu[:], in_=acc_k[:], func=ACT.Relu,
-                        bias=bn_shift[:, mk_tile : mk_tile + 1], scale=bn_scale[:, mk_tile : mk_tile + 1],
-                    )
-                    if total is None:
-                        total = relu
-                    else:
-                        longer = sum_pool.tile([P, 2, n], F32, tag="sum")
-                        nc.vector.tensor_add(out=longer[:], in0=total[:], in1=relu[:])
-                        total = longer
-                nc.vector.tensor_add(out=cells[:, m, out_cells], in0=total[:, 0, :], in1=total[:, 1, :])
-                for b in done:
-                    pool_image(image_cells(m, b), key_sums[:, mk_tile, b, :])
-                    store_key(b, mk_tile)
-
-        for block in range(BLOCKS):
-            codes = codes_pool.tile([P, PASSES, PLANES, BLOCK_CELLS], U32, tag="codes", align_bytes=64)
-            scales = codes_pool.tile([P, PASSES, PLANES, BLOCK_CELLS], U8, tag="scales", align_bytes=64)
-            grouped = []
-            for c in range(PASSES):
-                grouped_c = grouped_pool.tile([P, PLANES, BLOCK_CELLS, PACK], BF16, tag="grouped", align_bytes=64)
-                grouped.append(grouped_c)
-            for half, (lo, n) in enumerate(CHUNKS):
-                for c in range(PASSES):
-                    regroup(load_slab(2 * block + half, c), grouped[c], half)
-                for c in range(PASSES):
-                    for j in range(PLANES):
-                        nc.vector.quantize_mx(
-                            out=codes[:, c, j, lo : lo + n].bitcast(FP8X4),
-                            scales=scales[:, c, j, lo : lo + n],
-                            in_=grouped[c][:, j, lo : lo + n, :].rearrange("p w t -> p (w t)"),
-                        )
-                compute_chunk(codes, scales, block, lo, n)
+                pool_values(b)
+            add_planes(chunk, relus)
+            for b in done:
+                pool_and_store_keys(b)
+        for b in range(B):
+            store_values(b)

@@ -30,6 +30,7 @@ CELL_H, CELL_W = 2, 3
 PLANES = CELL_H * CELL_W
 CELL_COLS = W // CELL_W
 IMAGE_CELLS = (H // CELL_H) * CELL_COLS
+HALF_CELLS = IMAGE_CELLS // 2
 SLAB_ROWS = 16
 SLAB_CELL_ROWS = SLAB_ROWS // CELL_H
 SLAB_CELLS = SLAB_CELL_ROWS * CELL_COLS
@@ -256,33 +257,51 @@ def tile_afnb_pa_t_kernel(tc, low_feats, wk, bk, gk, bek, mk, vk, wv, bv, out_0,
         def level(sums, s):
             return sums[:, level_first[s] : level_first[s] + s * s]
 
-        def grid_sums(out, in_, s, side):
+        def grid_sums(out, in_, rows, cols, size):
             nc.vector.tensor_reduce(
-                out=out.rearrange("p (a c) -> p a c", a=s),
-                in_=in_.rearrange("p (a i c k) -> p a c i k", a=s, i=side // s, c=s, k=side // s),
+                out=out.rearrange("p (a c) -> p a c", a=rows),
+                in_=in_.rearrange("p (a i c k) -> p a c i k", a=rows, i=size, c=cols, k=size),
                 axis=AXIS.XY,
                 op=ALU.add,
             )
 
-        def pool_image(b, tiles):
+        def pool_half(half_image, tiles):
+            lower = half_image % 2
             for s in (8, 6):
                 for m, sums in tiles:
-                    grid_sums(level(sums, s), cells[:, m, b * IMAGE_CELLS : (b + 1) * IMAGE_CELLS], s, CELL_COLS)
-            for m, sums in tiles:
-                grid_sums(level(sums, 3), level(sums, 6), 3, 6)
-            for m, sums in tiles:
-                grid_sums(level(sums, 1), level(sums, 3), 1, 3)
+                    grid_sums(
+                        level(sums, s)[:, lower * (s * s // 2) : (lower + 1) * (s * s // 2)],
+                        cells[:, m, half_image * HALF_CELLS : (half_image + 1) * HALF_CELLS],
+                        s // 2, s, CELL_COLS // s,
+                    )
 
-        def pool_values(b):
-            pool_image(b, [(m, value_sums[:, m, b, :]) for m in range(V_TILES)])
-            nc.vector.tensor_add(out=value_sums[:, :, b, :], in0=value_sums[:, :, b, :], in1=bias_area[:])
+        def pool_coarse(tiles):
+            for m, sums in tiles:
+                grid_sums(level(sums, 3), level(sums, 6), 3, 3, 2)
+            for m, sums in tiles:
+                grid_sums(level(sums, 1), level(sums, 3), 1, 1, 3)
 
-        def pool_and_store_keys(b):
-            pool_image(b, [(V_TILES + mk_tile, key_sums[:, mk_tile, b, :]) for mk_tile in range(K_TILES)])
-            for mk_tile in range(K_TILES):
-                key_rows = out_pool.tile([P, LOCS], F32, tag="key_rows")
-                nc.vector.tensor_mul(out=key_rows[:], in0=key_sums[:, mk_tile, b, :], in1=inv_area_row[:, 0:LOCS])
-                nc.sync.dma_start(out=out_1[b, mk_tile * P : (mk_tile + 1) * P, :], in_=key_rows[:])
+        def pool_values(half_image):
+            b, lower = divmod(half_image, 2)
+            tiles = [(m, value_sums[:, m, b, :]) for m in range(V_TILES)]
+            pool_half(half_image, tiles)
+            if lower:
+                pool_coarse(tiles)
+                nc.vector.tensor_add(out=value_sums[:, :, b, :], in0=value_sums[:, :, b, :], in1=bias_area[:])
+
+        def pool_and_store_keys(half_image):
+            b, lower = divmod(half_image, 2)
+            tiles = [(V_TILES + mk_tile, key_sums[:, mk_tile, b, :]) for mk_tile in range(K_TILES)]
+            pool_half(half_image, tiles)
+            if lower:
+                pool_coarse(tiles)
+                key_rows = out_pool.tile([P, K_TILES, LOCS], F32, tag="key_rows")
+                nc.vector.tensor_mul(
+                    out=key_rows[:],
+                    in0=key_sums[:, :, b, :],
+                    in1=inv_area_row[:, 0:LOCS].unsqueeze(1).to_broadcast([P, K_TILES, LOCS]),
+                )
+                nc.sync.dma_start(out=out_1[b].rearrange("(m p) l -> p m l", p=P), in_=key_rows[:])
 
         def store_values(b):
             flipped = psum_k.tile([P, V_TILES, P], F32, tag="acc_k")
@@ -309,11 +328,11 @@ def tile_afnb_pa_t_kernel(tc, low_feats, wk, bk, gk, bek, mk, vk, wv, bv, out_0,
                 feed(chunk + AHEAD)
             relus = multiply(chunk)
             last_cell = (chunk // 2) * BLOCK_CELLS + sum(CHUNKS[chunk % 2])
-            done = [b for b in range(B) if last_cell - CHUNKS[chunk % 2][1] < (b + 1) * IMAGE_CELLS <= last_cell]
-            for b in done:
-                pool_values(b)
+            done = [h for h in range(2 * B) if last_cell - CHUNKS[chunk % 2][1] < (h + 1) * HALF_CELLS <= last_cell]
+            for half_image in done:
+                pool_values(half_image)
             add_planes(chunk, relus)
-            for b in done:
-                pool_and_store_keys(b)
+            for half_image in done:
+                pool_and_store_keys(half_image)
         for b in range(B):
             store_values(b)

@@ -40,7 +40,9 @@ BLOCKS = B * IMAGE_CELLS // BLOCK_CELLS
 CHUNKS = ((0, 128), (128, 256))
 SLABS = B * SLABS_PER_IMAGE
 AHEAD = 2
-RELU_BUFS = 9
+SUM_BUFS = 2 * K_TILES
+SCALAR_PLANES = 2
+TINY = 1e-30
 
 
 def tile_afnb_pa_t_kernel(tc, low_feats, wk, bk, gk, bek, mk, vk, wv, bv, out_0, out_1):
@@ -50,7 +52,7 @@ def tile_afnb_pa_t_kernel(tc, low_feats, wk, bk, gk, bek, mk, vk, wv, bv, out_0,
         raw_pool = stack.enter_context(tc.tile_pool(name="raw", bufs=2 * PASSES))
         grouped_pool = stack.enter_context(tc.tile_pool(name="grouped", bufs=2 * PASSES))
         codes_pool = stack.enter_context(tc.tile_pool(name="codes", bufs=2))
-        relu_pool = stack.enter_context(tc.tile_pool(name="relu", bufs=RELU_BUFS))
+        relu_pool = stack.enter_context(tc.tile_pool(name="relu", bufs=SUM_BUFS))
         out_pool = stack.enter_context(tc.tile_pool(name="out", bufs=2))
         psum_v = stack.enter_context(tc.psum_pool(name="psum_v", bufs=2))
         psum_k = stack.enter_context(tc.psum_pool(name="psum_k", bufs=6))
@@ -121,14 +123,36 @@ def tile_afnb_pa_t_kernel(tc, low_feats, wk, bk, gk, bek, mk, vk, wv, bv, out_0,
             nc.vector.tensor_scalar_mul(
                 out=bias_area[:, m, :], in0=area_row[:], scalar1=column("bv", V_TILES)[:, m : m + 1]
             )
+        sign = const.tile([P, K_TILES], F32)
+        nc.vector.tensor_scalar(
+            out=sign[:], in0=column("gk", K_TILES), scalar1=0.0, scalar2=2.0, op0=ALU.is_ge, op1=ALU.mult
+        )
+        nc.vector.tensor_scalar_add(out=sign[:], in0=sign[:], scalar1=-1.0)
+        abs_gk = const.tile([P, K_TILES], F32)
+        nc.vector.tensor_mul(out=abs_gk[:], in0=column("gk", K_TILES), in1=sign[:])
+        nc.vector.tensor_scalar_max(out=abs_gk[:], in0=abs_gk[:], scalar1=TINY)
+        inv_abs_gk = const.tile([P, K_TILES], F32)
+        nc.vector.reciprocal(out=inv_abs_gk[:], in_=abs_gk[:])
         inv_std = const.tile([P, K_TILES], F32)
         nc.vector.reciprocal(out=inv_std[:], in_=std[:])
-        bn_scale = const.tile([P, K_TILES], F32)
-        nc.vector.tensor_mul(out=bn_scale[:], in0=column("gk", K_TILES), in1=inv_std[:])
-        scaled = const.tile([P, K_TILES], F32)
-        nc.vector.tensor_mul(out=scaled[:], in0=centred[:], in1=bn_scale[:])
-        bn_shift = const.tile([P, K_TILES], F32)
-        nc.vector.tensor_add(out=bn_shift[:], in0=scaled[:], in1=column("bek", K_TILES))
+        abs_scale = const.tile([P, K_TILES], F32)
+        nc.vector.tensor_mul(out=abs_scale[:], in0=abs_gk[:], in1=inv_std[:])
+        inv_abs_scale = const.tile([P, K_TILES], F32)
+        nc.vector.tensor_mul(out=inv_abs_scale[:], in0=std[:], in1=inv_abs_gk[:])
+        neg_theta = const.tile([P, K_TILES], F32)
+        nc.vector.tensor_mul(out=neg_theta[:], in0=centred[:], in1=sign[:])
+        bek_part = const.tile([P, K_TILES], F32)
+        nc.vector.tensor_mul(out=bek_part[:], in0=column("bek", K_TILES), in1=inv_abs_scale[:])
+        nc.vector.tensor_add(out=neg_theta[:], in0=neg_theta[:], in1=bek_part[:])
+        theta = const.tile([P, K_TILES], F32)
+        nc.vector.tensor_scalar_mul(out=theta[:], in0=neg_theta[:], scalar1=-1.0)
+        surplus = const.tile([P, K_TILES], F32)
+        nc.vector.tensor_scalar_mul(out=surplus[:], in0=neg_theta[:], scalar1=float(PLANES - SCALAR_PLANES))
+        key_factor = const.tile([P, K_TILES, LOCS], F32)
+        for mk_tile in range(K_TILES):
+            nc.vector.tensor_scalar_mul(
+                out=key_factor[:, mk_tile, :], in0=inv_area_row[:, 0:LOCS], scalar1=abs_scale[:, mk_tile : mk_tile + 1]
+            )
 
         cells = const.tile([P, W_TILES, B * IMAGE_CELLS], F32)
         value_sums = const.tile([P, V_TILES, B, P], F32)
@@ -139,6 +163,10 @@ def tile_afnb_pa_t_kernel(tc, low_feats, wk, bk, gk, bek, mk, vk, wv, bv, out_0,
         w_scales = const.tile([P, W_TILES, PASSES, P], U8, align_bytes=64)
 
         def quantise_weights():
+            for mk_tile in range(K_TILES):
+                nc.vector.tensor_scalar_mul(
+                    out=w_raws[1][:, mk_tile, :], in0=w_raws[1][:, mk_tile, :], scalar1=sign[:, mk_tile : mk_tile + 1]
+                )
             w_grouped = grouped_pool.tile([P, W_TILES, PASSES, P, PACK], BF16, tag="grouped", align_bytes=64)
             w_grouped_words = w_grouped[:].bitcast(F32)
             m = 0
@@ -222,10 +250,10 @@ def tile_afnb_pa_t_kernel(tc, low_feats, wk, bk, gk, bek, mk, vk, wv, bv, out_0,
                                 start=(c == 0 and j == 0), stop=(c == PASSES - 1 and j == PLANES - 1),
                             )
                 nc.scalar.copy(out=cells[:, 2 * pair : 2 * pair + 2, first_cell : first_cell + n], in_=acc_v[:])
-            relus = []
-            for mk_tile in range(K_TILES):
-                relus.append([])
-                for pair in range(PLANES // 2):
+            sums = []
+            waiting = []
+            for pair in range(PLANES // 2):
+                for mk_tile in range(K_TILES):
                     acc_k = psum_k.tile([P, 2, n], F32, tag="acc_k")
                     for i in range(2):
                         for c in range(PASSES):
@@ -233,25 +261,30 @@ def tile_afnb_pa_t_kernel(tc, low_feats, wk, bk, gk, bek, mk, vk, wv, bv, out_0,
                                 acc_k[:, i, :], V_TILES + mk_tile, c, 2 * pair + i,
                                 start=(c == 0), stop=(c == PASSES - 1),
                             )
-                    relu = relu_pool.tile([P, 2, n], F32, tag="relu")
-                    nc.scalar.activation(
-                        out=relu[:], in_=acc_k[:], func=ACT.Relu,
-                        bias=bn_shift[:, mk_tile : mk_tile + 1], scale=bn_scale[:, mk_tile : mk_tile + 1],
-                    )
-                    relus[mk_tile].append(relu)
-            return relus
+                    if pair == 0:
+                        plane_sum = relu_pool.tile([P, 2, n], F32, tag="relu")
+                        nc.scalar.activation(
+                            out=plane_sum[:], in_=acc_k[:], func=ACT.Relu, bias=neg_theta[:, mk_tile : mk_tile + 1]
+                        )
+                        sums.append(plane_sum)
+                    else:
+                        waiting.append((mk_tile, acc_k))
+            return sums, waiting
 
-        def add_planes(chunk, relus):
+        def add_planes(chunk, sums, waiting):
             block, half = divmod(chunk, 2)
             lo, n = CHUNKS[half]
             first_cell = block * BLOCK_CELLS + lo
-            for pair in range(1, PLANES // 2):
-                for planes in relus:
-                    nc.vector.tensor_add(out=planes[0][:], in0=planes[0][:], in1=planes[pair][:])
-            for mk_tile, planes in enumerate(relus):
-                nc.vector.tensor_add(
+            for mk_tile, acc_k in waiting:
+                nc.vector.scalar_tensor_tensor(
+                    out=sums[mk_tile][:], in0=acc_k[:], scalar=theta[:, mk_tile : mk_tile + 1], in1=sums[mk_tile][:],
+                    op0=ALU.max, op1=ALU.add,
+                )
+            for mk_tile, plane_sum in enumerate(sums):
+                nc.vector.scalar_tensor_tensor(
                     out=cells[:, V_TILES + mk_tile, first_cell : first_cell + n],
-                    in0=planes[0][:, 0, :], in1=planes[0][:, 1, :],
+                    in0=plane_sum[:, 0, :], scalar=surplus[:, mk_tile : mk_tile + 1], in1=plane_sum[:, 1, :],
+                    op0=ALU.add, op1=ALU.add,
                 )
 
         def level(sums, s):
@@ -296,11 +329,7 @@ def tile_afnb_pa_t_kernel(tc, low_feats, wk, bk, gk, bek, mk, vk, wv, bv, out_0,
             if lower:
                 pool_coarse(tiles)
                 key_rows = out_pool.tile([P, K_TILES, LOCS], F32, tag="key_rows")
-                nc.vector.tensor_mul(
-                    out=key_rows[:],
-                    in0=key_sums[:, :, b, :],
-                    in1=inv_area_row[:, 0:LOCS].unsqueeze(1).to_broadcast([P, K_TILES, LOCS]),
-                )
+                nc.vector.tensor_mul(out=key_rows[:], in0=key_sums[:, :, b, :], in1=key_factor[:])
                 nc.sync.dma_start(out=out_1[b].rearrange("(m p) l -> p m l", p=P), in_=key_rows[:])
 
         def store_values(b):
@@ -326,12 +355,12 @@ def tile_afnb_pa_t_kernel(tc, low_feats, wk, bk, gk, bek, mk, vk, wv, bv, out_0,
                 if chunk + AHEAD + 1 < SLABS:
                     load_slab(chunk + AHEAD + 1)
                 feed(chunk + AHEAD)
-            relus = multiply(chunk)
+            sums, waiting = multiply(chunk)
             last_cell = (chunk // 2) * BLOCK_CELLS + sum(CHUNKS[chunk % 2])
             done = [h for h in range(2 * B) if last_cell - CHUNKS[chunk % 2][1] < (h + 1) * HALF_CELLS <= last_cell]
             for half_image in done:
                 pool_values(half_image)
-            add_planes(chunk, relus)
+            add_planes(chunk, sums, waiting)
             for half_image in done:
                 pool_and_store_keys(half_image)
         for b in range(B):

@@ -43,6 +43,7 @@ AHEAD = 2
 SUM_BUFS = 2 * K_TILES
 SCALAR_PLANES = 2
 TINY = 1e-30
+VECTOR_ROWS = (8, 6)
 
 
 def tile_afnb_pa_t_kernel(tc, low_feats, wk, bk, gk, bek, mk, vk, wv, bv, out_0, out_1):
@@ -118,11 +119,8 @@ def tile_afnb_pa_t_kernel(tc, low_feats, wk, bk, gk, bek, mk, vk, wv, bv, out_0,
         nc.scalar.activation(out=std[:], in_=var_eps[:], func=ACT.Sqrt)
         centred = const.tile([P, K_TILES], F32)
         nc.vector.tensor_sub(out=centred[:], in0=column("bk", K_TILES), in1=column("mk", K_TILES))
-        bias_area = const.tile([P, V_TILES, P], F32)
-        for m in range(V_TILES):
-            nc.vector.tensor_scalar_mul(
-                out=bias_area[:, m, :], in0=area_row[:], scalar1=column("bv", V_TILES)[:, m : m + 1]
-            )
+        cell_bias = const.tile([P, V_TILES], F32)
+        nc.vector.tensor_scalar_mul(out=cell_bias[:], in0=column("bv", V_TILES), scalar1=float(PLANES))
         sign = const.tile([P, K_TILES], F32)
         nc.vector.tensor_scalar(
             out=sign[:], in0=column("gk", K_TILES), scalar1=0.0, scalar2=2.0, op0=ALU.is_ge, op1=ALU.mult
@@ -177,8 +175,7 @@ def tile_afnb_pa_t_kernel(tc, low_feats, wk, bk, gk, bek, mk, vk, wv, bv, out_0,
                     for c in range(PASSES):
                         for u in range(2):
                             nc.tensor.transpose(out=flipped[:, c, u, :], in_=words[:, i, c, u, :], identity=ident[:])
-                    copy = nc.vector.tensor_copy if m % 2 == 0 else nc.scalar.copy
-                    copy(out=w_grouped_words[:, m], in_=flipped[:].rearrange("p c u r -> p c r u"))
+                    nc.scalar.copy(out=w_grouped_words[:, m], in_=flipped[:].rearrange("p c u r -> p c r u"))
                     m += 1
             for m in range(W_TILES):
                 nc.vector.quantize_mx(
@@ -187,7 +184,7 @@ def tile_afnb_pa_t_kernel(tc, low_feats, wk, bk, gk, bek, mk, vk, wv, bv, out_0,
                     in_=w_grouped[:, m].rearrange("p c r t -> p (c r t)"),
                 )
 
-        def regroup(raw, grouped, half):
+        def regroup(raw, grouped, half, vector_rows):
             src = raw[:].rearrange(
                 "p t (hi jh cp i jw) -> p jh hi cp t i jw",
                 hi=SLAB_CELL_ROWS, jh=CELL_H, cp=CELL_COLS // 2, i=2, jw=CELL_W,
@@ -196,7 +193,9 @@ def tile_afnb_pa_t_kernel(tc, low_feats, wk, bk, gk, bek, mk, vk, wv, bv, out_0,
                 "p (jh jw) (hi cp i) t -> p jh hi cp t i jw",
                 jh=CELL_H, jw=CELL_W, hi=SLAB_CELL_ROWS, cp=CELL_COLS // 2, i=2,
             )
-            nc.vector.tensor_copy(out=dst[:, 0], in_=src[:, 0])
+            nc.vector.tensor_copy(out=dst[:, 0, 0:vector_rows], in_=src[:, 0, 0:vector_rows])
+            if vector_rows < SLAB_CELL_ROWS:
+                nc.scalar.copy(out=dst[:, 0, vector_rows:], in_=src[:, 0, vector_rows:])
             nc.scalar.copy(out=dst[:, 1], in_=src[:, 1])
 
         blocks = {}
@@ -213,7 +212,7 @@ def tile_afnb_pa_t_kernel(tc, low_feats, wk, bk, gk, bek, mk, vk, wv, bv, out_0,
                 blocks[block] = (grouped, codes, scales)
             grouped, codes, scales = blocks[block]
             for c in range(PASSES):
-                regroup(raws[slab][c], grouped[c], half)
+                regroup(raws[slab][c], grouped[c], half, VECTOR_ROWS[c])
             lo, n = CHUNKS[half]
             for c in range(PASSES):
                 for j in range(PLANES):
@@ -249,7 +248,11 @@ def tile_afnb_pa_t_kernel(tc, low_feats, wk, bk, gk, bek, mk, vk, wv, bv, out_0,
                                 acc_v[:, i, :], 2 * pair + i, c, j,
                                 start=(c == 0 and j == 0), stop=(c == PASSES - 1 and j == PLANES - 1),
                             )
-                nc.scalar.copy(out=cells[:, 2 * pair : 2 * pair + 2, first_cell : first_cell + n], in_=acc_v[:])
+                for i in range(2):
+                    nc.scalar.activation(
+                        out=cells[:, 2 * pair + i, first_cell : first_cell + n], in_=acc_v[:, i, :], func=ACT.Identity,
+                        bias=cell_bias[:, 2 * pair + i : 2 * pair + i + 1],
+                    )
             sums = []
             waiting = []
             for pair in range(PLANES // 2):
@@ -320,7 +323,6 @@ def tile_afnb_pa_t_kernel(tc, low_feats, wk, bk, gk, bek, mk, vk, wv, bv, out_0,
             pool_half(half_image, tiles)
             if lower:
                 pool_coarse(tiles)
-                nc.vector.tensor_add(out=value_sums[:, :, b, :], in0=value_sums[:, :, b, :], in1=bias_area[:])
 
         def pool_and_store_keys(half_image):
             b, lower = divmod(half_image, 2)

@@ -31,26 +31,32 @@ PLANES = CELL_H * CELL_W
 CELL_COLS = W // CELL_W
 IMAGE_CELLS = (H // CELL_H) * CELL_COLS
 HALF_CELLS = IMAGE_CELLS // 2
-SLAB_ROWS = 16
-SLAB_CELL_ROWS = SLAB_ROWS // CELL_H
-SLAB_CELLS = SLAB_CELL_ROWS * CELL_COLS
-SLABS_PER_IMAGE = H // SLAB_ROWS
-BLOCK_CELLS = 2 * SLAB_CELLS
-BLOCKS = B * IMAGE_CELLS // BLOCK_CELLS
-CHUNKS = ((0, 128), (128, 256))
-SLABS = B * SLABS_PER_IMAGE
-AHEAD = 2
+STRIP_CELL_ROWS = 4
+STRIP_ROWS = STRIP_CELL_ROWS * CELL_H
+STRIP_CELLS = STRIP_CELL_ROWS * CELL_COLS
+STRIPS_PER_IMAGE = H // STRIP_ROWS
+STRIPS = B * STRIPS_PER_IMAGE
+BLOCK_STRIPS = 4
+BLOCK_CELLS = BLOCK_STRIPS * STRIP_CELLS
+CHUNKS = ((0, 0, 128), (0, 128, 256), (1, 0, 128), (1, 128, 256), (2, 0, 128), (2, 128, 256))
+LOADS = (2, 2, 2, 2, 2, 2)
+RAW_BUFS = 6
 SUM_BUFS = 2 * K_TILES
 SCALAR_PLANES = 2
 TINY = 1e-30
-VECTOR_ROWS = (8, 6)
+VECTOR_PIECES = (((0, 0), (1, 0)), ((0, 0), (1, 0)), ((0, 0), (1, 0)), ((0, 0), (1, 0)), ((0, 0), (1, 0)), ((0, 0), (1, 0)), ((0, 0), (1, 0)), ((0, 0), (1, 0)), ((0, 0),), ((0, 0),), ((0, 0),), ((0, 0),),)
+Q_AHEAD = 2
+S_FILL = (1, 1, 1, 1)
+V_FILL = 2
+POOL_LAG = 0
+HEAD = ("x", "w", "x")
 
 
 def tile_afnb_pa_t_kernel(tc, low_feats, wk, bk, gk, bek, mk, vk, wv, bv, out_0, out_1):
     nc = tc.nc
     with ExitStack() as stack:
         const = stack.enter_context(tc.tile_pool(name="const", bufs=1))
-        raw_pool = stack.enter_context(tc.tile_pool(name="raw", bufs=2 * PASSES))
+        raw_pool = stack.enter_context(tc.tile_pool(name="raw", bufs=RAW_BUFS))
         grouped_pool = stack.enter_context(tc.tile_pool(name="grouped", bufs=2 * PASSES))
         codes_pool = stack.enter_context(tc.tile_pool(name="codes", bufs=2))
         relu_pool = stack.enter_context(tc.tile_pool(name="relu", bufs=SUM_BUFS))
@@ -58,16 +64,20 @@ def tile_afnb_pa_t_kernel(tc, low_feats, wk, bk, gk, bek, mk, vk, wv, bv, out_0,
         psum_v = stack.enter_context(tc.psum_pool(name="psum_v", bufs=2))
         psum_k = stack.enter_context(tc.psum_pool(name="psum_k", bufs=6))
 
-        raws = {}
+        strip_raw = {}
 
-        def load_slab(slab):
-            b, part = divmod(slab, SLABS_PER_IMAGE)
-            raws[slab] = []
+        def load(index):
+            first = sum(LOADS[:index])
+            count = LOADS[index]
+            b, part = divmod(first, STRIPS_PER_IMAGE)
+            tiles = []
             for c in range(PASSES):
-                raw = raw_pool.tile([P, PACK, SLAB_ROWS * W], BF16, tag="raw")
-                rows = low_feats[b, c * K_PASS : (c + 1) * K_PASS, part * SLAB_ROWS : (part + 1) * SLAB_ROWS, :]
+                raw = raw_pool.tile([P, PACK, count * STRIP_ROWS * W], BF16, tag="raw")
+                rows = low_feats[b, c * K_PASS : (c + 1) * K_PASS, part * STRIP_ROWS : (part + count) * STRIP_ROWS, :]
                 nc.sync.dma_start(out=raw[:], in_=rows.rearrange("(p t) h w -> p t (h w)", t=PACK))
-                raws[slab].append(raw)
+                tiles.append(raw)
+            for k in range(count):
+                strip_raw[first + k] = (tiles, k * STRIP_CELL_ROWS, count * STRIP_CELL_ROWS)
 
         vector_rows = const.tile([P, P], BF16)
         nc.vector.memset(vector_rows[:], 0.0)
@@ -78,12 +88,30 @@ def tile_afnb_pa_t_kernel(tc, low_feats, wk, bk, gk, bek, mk, vk, wv, bv, out_0,
             nc.scalar.dma_start(out=vector_rows[row : row + rows, :], in_=vector.rearrange("(r c) -> r c", c=P))
             first_row[name] = row
             row += rows
-        load_slab(0)
+
         w_raws = []
-        for w_dram, count in ((wv, V_TILES), (wk, K_TILES)):
-            w_raw = raw_pool.tile([P, count, CL], BF16, tag="raw")
-            nc.sync.dma_start(out=w_raw[:], in_=w_dram.rearrange("(m p) k -> p m k", p=P))
-            w_raws.append(w_raw)
+
+        def load_weights():
+            for w_dram, count in ((wv, V_TILES), (wk, K_TILES)):
+                w_raw = raw_pool.tile([P, count, CL], BF16, tag="raw")
+                nc.sync.dma_start(out=w_raw[:], in_=w_dram.rearrange("(m p) k -> p m k", p=P))
+                w_raws.append(w_raw)
+
+        taken = []
+        next_load = [0]
+        weights_read = [False]
+
+        def load_next():
+            load(next_load[0])
+            next_load[0] += 1
+            taken.append(sum(LOADS[: next_load[0]]))
+
+        for what in HEAD:
+            if what == "w":
+                load_weights()
+                taken.append("w")
+            else:
+                load_next()
 
         ident = const.tile([P, P], F32)
         make_identity(nc, ident[:])
@@ -119,8 +147,6 @@ def tile_afnb_pa_t_kernel(tc, low_feats, wk, bk, gk, bek, mk, vk, wv, bv, out_0,
         nc.scalar.activation(out=std[:], in_=var_eps[:], func=ACT.Sqrt)
         centred = const.tile([P, K_TILES], F32)
         nc.vector.tensor_sub(out=centred[:], in0=column("bk", K_TILES), in1=column("mk", K_TILES))
-        cell_bias = const.tile([P, V_TILES], F32)
-        nc.vector.tensor_scalar_mul(out=cell_bias[:], in0=column("bv", V_TILES), scalar1=float(PLANES))
         sign = const.tile([P, K_TILES], F32)
         nc.vector.tensor_scalar(
             out=sign[:], in0=column("gk", K_TILES), scalar1=0.0, scalar2=2.0, op0=ALU.is_ge, op1=ALU.mult
@@ -151,12 +177,15 @@ def tile_afnb_pa_t_kernel(tc, low_feats, wk, bk, gk, bek, mk, vk, wv, bv, out_0,
             nc.vector.tensor_scalar_mul(
                 out=key_factor[:, mk_tile, :], in0=inv_area_row[:, 0:LOCS], scalar1=abs_scale[:, mk_tile : mk_tile + 1]
             )
+        cell_bias = const.tile([P, V_TILES], F32)
+        nc.vector.tensor_scalar_mul(out=cell_bias[:], in0=column("bv", V_TILES), scalar1=float(PLANES))
 
         cells = const.tile([P, W_TILES, B * IMAGE_CELLS], F32)
         value_sums = const.tile([P, V_TILES, B, P], F32)
         nc.vector.memset(value_sums[:, :, :, LOCS:], 0.0)
         key_sums = const.tile([P, K_TILES, B, LOCS], F32)
 
+        w_grouped = grouped_pool.tile([P, W_TILES, PASSES, P, PACK], BF16, tag="grouped", align_bytes=64)
         w_codes = const.tile([P, W_TILES, PASSES, P], U32, align_bytes=64)
         w_scales = const.tile([P, W_TILES, PASSES, P], U8, align_bytes=64)
 
@@ -165,7 +194,6 @@ def tile_afnb_pa_t_kernel(tc, low_feats, wk, bk, gk, bek, mk, vk, wv, bv, out_0,
                 nc.vector.tensor_scalar_mul(
                     out=w_raws[1][:, mk_tile, :], in0=w_raws[1][:, mk_tile, :], scalar1=sign[:, mk_tile : mk_tile + 1]
                 )
-            w_grouped = grouped_pool.tile([P, W_TILES, PASSES, P, PACK], BF16, tag="grouped", align_bytes=64)
             w_grouped_words = w_grouped[:].bitcast(F32)
             m = 0
             for w_raw, count in zip(w_raws, (V_TILES, K_TILES)):
@@ -177,6 +205,7 @@ def tile_afnb_pa_t_kernel(tc, low_feats, wk, bk, gk, bek, mk, vk, wv, bv, out_0,
                             nc.tensor.transpose(out=flipped[:, c, u, :], in_=words[:, i, c, u, :], identity=ident[:])
                     nc.scalar.copy(out=w_grouped_words[:, m], in_=flipped[:].rearrange("p c u r -> p c r u"))
                     m += 1
+            weights_read[0] = True
             for m in range(W_TILES):
                 nc.vector.quantize_mx(
                     out=w_codes[:, m].rearrange("p c r -> p (c r)").bitcast(FP8X4),
@@ -184,36 +213,79 @@ def tile_afnb_pa_t_kernel(tc, low_feats, wk, bk, gk, bek, mk, vk, wv, bv, out_0,
                     in_=w_grouped[:, m].rearrange("p c r t -> p (c r t)"),
                 )
 
-        def regroup(raw, grouped, half, vector_rows):
-            src = raw[:].rearrange(
-                "p t (hi jh cp i jw) -> p jh hi cp t i jw",
-                hi=SLAB_CELL_ROWS, jh=CELL_H, cp=CELL_COLS // 2, i=2, jw=CELL_W,
-            )
-            dst = grouped[:, :, half * SLAB_CELLS : (half + 1) * SLAB_CELLS, :].rearrange(
-                "p (jh jw) (hi cp i) t -> p jh hi cp t i jw",
-                jh=CELL_H, jw=CELL_W, hi=SLAB_CELL_ROWS, cp=CELL_COLS // 2, i=2,
-            )
-            nc.vector.tensor_copy(out=dst[:, 0, 0:vector_rows], in_=src[:, 0, 0:vector_rows])
-            if vector_rows < SLAB_CELL_ROWS:
-                nc.scalar.copy(out=dst[:, 0, vector_rows:], in_=src[:, 0, vector_rows:])
-            nc.scalar.copy(out=dst[:, 1], in_=src[:, 1])
-
         blocks = {}
 
-        def feed(slab):
-            block, half = divmod(slab, 2)
-            if half == 0:
-                codes = codes_pool.tile([P, PASSES, PLANES, BLOCK_CELLS], U32, tag="codes", align_bytes=64)
-                scales = codes_pool.tile([P, PASSES, PLANES, BLOCK_CELLS], U8, tag="scales", align_bytes=64)
-                grouped = []
+        groupeds = {}
+
+        def grouped_tiles(block):
+            if block not in groupeds:
+                groupeds[block] = []
                 for c in range(PASSES):
                     grouped_c = grouped_pool.tile([P, PLANES, BLOCK_CELLS, PACK], BF16, tag="grouped", align_bytes=64)
-                    grouped.append(grouped_c)
-                blocks[block] = (grouped, codes, scales)
-            grouped, codes, scales = blocks[block]
+                    groupeds[block].append(grouped_c)
+            return groupeds[block]
+
+        def code_tiles(block):
+            if block not in blocks:
+                codes = codes_pool.tile([P, PASSES, PLANES, BLOCK_CELLS], U32, tag="codes", align_bytes=64)
+                scales = codes_pool.tile([P, PASSES, PLANES, BLOCK_CELLS], U8, tag="scales", align_bytes=64)
+                blocks[block] = (codes, scales)
+            return blocks[block]
+
+        def regroup(strip, c, jh, copy):
+            tiles, first_cell_row, cell_rows = strip_raw[strip]
+            block, part = divmod(strip, BLOCK_STRIPS)
+            grouped = grouped_tiles(block)[c]
+            src = tiles[c][:].rearrange(
+                "p t (hi jh cp i jw) -> p jh hi cp t i jw", hi=cell_rows, jh=CELL_H, cp=CELL_COLS // 2, i=2, jw=CELL_W
+            )
+            dst = grouped[:, :, part * STRIP_CELLS : (part + 1) * STRIP_CELLS, :].rearrange(
+                "p (jh jw) (hi cp i) t -> p jh hi cp t i jw",
+                jh=CELL_H, jw=CELL_W, hi=STRIP_CELL_ROWS, cp=CELL_COLS // 2, i=2,
+            )
+            copy(out=dst[:, jh], in_=src[:, jh, first_cell_row : first_cell_row + STRIP_CELL_ROWS])
+
+        scalar_pieces = []
+        vector_pieces = []
+        for strip in range(STRIPS):
             for c in range(PASSES):
-                regroup(raws[slab][c], grouped[c], half, VECTOR_ROWS[c])
-            lo, n = CHUNKS[half]
+                for jh in range(CELL_H):
+                    if (c, jh) in VECTOR_PIECES[strip % len(VECTOR_PIECES)]:
+                        vector_pieces.append((strip, c, jh))
+                    else:
+                        scalar_pieces.append((strip, c, jh))
+        loaded = [0]
+        released = [0]
+
+        def emit(pieces, copy, count, below=STRIPS):
+            while count > 0 and pieces and pieces[0][0] < below:
+                strip, c, jh = pieces[0]
+                if strip not in strip_raw:
+                    break
+                pieces.remove(pieces[0])
+                regroup(strip, c, jh, copy)
+                count -= 1
+            done = min([p[0][0] if p else STRIPS for p in (scalar_pieces, vector_pieces)])
+            while next_load[0] < len(LOADS):
+                old = taken[len(taken) - RAW_BUFS // PASSES]
+                if (old == "w" and not weights_read[0]) or (old != "w" and old > done):
+                    break
+                load_next()
+
+        def scalar_fill(count, below=STRIPS):
+            emit(scalar_pieces, nc.scalar.copy, count, below)
+
+        def vector_fill(count, below=STRIPS):
+            emit(vector_pieces, nc.vector.tensor_copy, count, below)
+
+        def quantise(chunk):
+            block, lo, n = CHUNKS[chunk]
+            strips = block * BLOCK_STRIPS + -(-(lo + n) // STRIP_CELLS)
+            for turn in range(STRIPS * PASSES * CELL_H):
+                scalar_fill(1, strips)
+                vector_fill(1, strips)
+            grouped = grouped_tiles(block)
+            codes, scales = code_tiles(block)
             for c in range(PASSES):
                 for j in range(PLANES):
                     nc.vector.quantize_mx(
@@ -222,62 +294,59 @@ def tile_afnb_pa_t_kernel(tc, low_feats, wk, bk, gk, bek, mk, vk, wv, bv, out_0,
                         in_=grouped[c][:, j, lo : lo + n, :].rearrange("p w t -> p (w t)"),
                     )
 
-        def multiply(chunk):
-            block, half = divmod(chunk, 2)
-            grouped, codes, scales = blocks[block]
-            lo, n = CHUNKS[half]
-            first_cell = block * BLOCK_CELLS + lo
+        def mx_pass(chunk, acc, m, c, j, start, stop):
+            block, lo, n = CHUNKS[chunk]
+            codes, scales = blocks[block]
+            nc.tensor.matmul_mx(
+                out=acc,
+                lhsT=w_codes[:, m, c, :].bitcast(FP8X4),
+                lhsT_scale=w_scales[:, m, c, :],
+                rhs=codes[:, c, j, lo : lo + n].bitcast(FP8X4),
+                rhs_scale=scales[:, c, j, lo : lo + n],
+                start=start,
+                stop=stop,
+            )
 
-            def mx_pass(acc, m, c, j, start, stop):
-                nc.tensor.matmul_mx(
-                    out=acc,
-                    lhsT=w_codes[:, m, c, :].bitcast(FP8X4),
-                    lhsT_scale=w_scales[:, m, c, :],
-                    rhs=codes[:, c, j, lo : lo + n].bitcast(FP8X4),
-                    rhs_scale=scales[:, c, j, lo : lo + n],
-                    start=start,
-                    stop=stop,
+        def first_cell(chunk):
+            block, lo, n = CHUNKS[chunk]
+            return block * BLOCK_CELLS + lo
+
+        def values(chunk, pair):
+            n = CHUNKS[chunk][2]
+            acc_v = psum_v.tile([P, 2, n], F32, tag="acc_v")
+            for i in range(2):
+                for c in range(PASSES):
+                    for j in range(PLANES):
+                        mx_pass(
+                            chunk, acc_v[:, i, :], 2 * pair + i, c, j,
+                            start=(c == 0 and j == 0), stop=(c == PASSES - 1 and j == PLANES - 1),
+                        )
+            return acc_v
+
+        def values_out(chunk, pair, acc_v):
+            n = CHUNKS[chunk][2]
+            for i in range(2):
+                nc.scalar.activation(
+                    out=cells[:, 2 * pair + i, first_cell(chunk) : first_cell(chunk) + n], in_=acc_v[:, i, :], func=ACT.Identity,
+                    bias=cell_bias[:, 2 * pair + i : 2 * pair + i + 1],
                 )
 
-            for pair in range(V_TILES // 2):
-                acc_v = psum_v.tile([P, 2, n], F32, tag="acc_v")
-                for i in range(2):
-                    for c in range(PASSES):
-                        for j in range(PLANES):
-                            mx_pass(
-                                acc_v[:, i, :], 2 * pair + i, c, j,
-                                start=(c == 0 and j == 0), stop=(c == PASSES - 1 and j == PLANES - 1),
-                            )
-                for i in range(2):
-                    nc.scalar.activation(
-                        out=cells[:, 2 * pair + i, first_cell : first_cell + n], in_=acc_v[:, i, :], func=ACT.Identity,
-                        bias=cell_bias[:, 2 * pair + i : 2 * pair + i + 1],
-                    )
-            sums = []
-            waiting = []
-            for pair in range(PLANES // 2):
-                for mk_tile in range(K_TILES):
-                    acc_k = psum_k.tile([P, 2, n], F32, tag="acc_k")
-                    for i in range(2):
-                        for c in range(PASSES):
-                            mx_pass(
-                                acc_k[:, i, :], V_TILES + mk_tile, c, 2 * pair + i,
-                                start=(c == 0), stop=(c == PASSES - 1),
-                            )
-                    if pair == 0:
-                        plane_sum = relu_pool.tile([P, 2, n], F32, tag="relu")
-                        nc.scalar.activation(
-                            out=plane_sum[:], in_=acc_k[:], func=ACT.Relu, bias=neg_theta[:, mk_tile : mk_tile + 1]
-                        )
-                        sums.append(plane_sum)
-                    else:
-                        waiting.append((mk_tile, acc_k))
-            return sums, waiting
+        def keys(chunk, pair, mk_tile):
+            n = CHUNKS[chunk][2]
+            acc_k = psum_k.tile([P, 2, n], F32, tag="acc_k")
+            for i in range(2):
+                for c in range(PASSES):
+                    mx_pass(chunk, acc_k[:, i, :], V_TILES + mk_tile, c, 2 * pair + i, start=(c == 0), stop=(c == PASSES - 1))
+            return acc_k
+
+        def begin_sum(chunk, mk_tile, acc_k):
+            n = CHUNKS[chunk][2]
+            plane_sum = relu_pool.tile([P, 2, n], F32, tag="relu")
+            nc.scalar.activation(out=plane_sum[:], in_=acc_k[:], func=ACT.Relu, bias=neg_theta[:, mk_tile : mk_tile + 1])
+            return plane_sum
 
         def add_planes(chunk, sums, waiting):
-            block, half = divmod(chunk, 2)
-            lo, n = CHUNKS[half]
-            first_cell = block * BLOCK_CELLS + lo
+            n = CHUNKS[chunk][2]
             for mk_tile, acc_k in waiting:
                 nc.vector.scalar_tensor_tensor(
                     out=sums[mk_tile][:], in0=acc_k[:], scalar=theta[:, mk_tile : mk_tile + 1], in1=sums[mk_tile][:],
@@ -285,7 +354,7 @@ def tile_afnb_pa_t_kernel(tc, low_feats, wk, bk, gk, bek, mk, vk, wv, bv, out_0,
                 )
             for mk_tile, plane_sum in enumerate(sums):
                 nc.vector.scalar_tensor_tensor(
-                    out=cells[:, V_TILES + mk_tile, first_cell : first_cell + n],
+                    out=cells[:, V_TILES + mk_tile, first_cell(chunk) : first_cell(chunk) + n],
                     in0=plane_sum[:, 0, :], scalar=surplus[:, mk_tile : mk_tile + 1], in1=plane_sum[:, 1, :],
                     op0=ALU.add, op1=ALU.add,
                 )
@@ -323,6 +392,7 @@ def tile_afnb_pa_t_kernel(tc, low_feats, wk, bk, gk, bek, mk, vk, wv, bv, out_0,
             pool_half(half_image, tiles)
             if lower:
                 pool_coarse(tiles)
+                to_store.append(b)
 
         def pool_and_store_keys(half_image):
             b, lower = divmod(half_image, 2)
@@ -335,35 +405,76 @@ def tile_afnb_pa_t_kernel(tc, low_feats, wk, bk, gk, bek, mk, vk, wv, bv, out_0,
                 nc.sync.dma_start(out=out_1[b].rearrange("(m p) l -> p m l", p=P), in_=key_rows[:])
 
         def store_values(b):
-            flipped = psum_k.tile([P, V_TILES, P], F32, tag="acc_k")
+            flipped = psum_v.tile([P, V_TILES, P], F32, tag="acc_v")
             for m in range(V_TILES):
                 nc.tensor.transpose(out=flipped[:, m, :], in_=value_sums[:, m, b, :], identity=ident[:])
             value_rows = out_pool.tile([P, CV], F32, tag="value_rows")
             nc.scalar.activation(
-                out=value_rows[:],
-                in_=flipped[:].rearrange("p m r -> p (m r)"),
-                func=ACT.Copy,
-                scale=inv_area_col[:, 0:1],
+                out=value_rows[:], in_=flipped[:].rearrange("p m r -> p (m r)"), func=ACT.Copy, scale=inv_area_col[:, 0:1]
             )
             nc.sync.dma_start(out=out_0[b], in_=value_rows[0:LOCS, :])
 
-        feed(0)
-        load_slab(1)
+        def halves_done(chunk):
+            n = CHUNKS[chunk][2]
+            last_cell = first_cell(chunk) + n
+            return [h for h in range(2 * B) if last_cell - n < (h + 1) * HALF_CELLS <= last_cell]
+
+        quantised = [0]
+        to_store = []
+
+        def quantise_up_to(chunk):
+            while quantised[0] <= min(chunk, len(CHUNKS) - 1):
+                quantise(quantised[0])
+                quantised[0] += 1
+
+        quantise_up_to(0)
         quantise_weights()
-        load_slab(2)
-        feed(1)
-        for chunk in range(SLABS):
-            if chunk + AHEAD < SLABS:
-                if chunk + AHEAD + 1 < SLABS:
-                    load_slab(chunk + AHEAD + 1)
-                feed(chunk + AHEAD)
-            sums, waiting = multiply(chunk)
-            last_cell = (chunk // 2) * BLOCK_CELLS + sum(CHUNKS[chunk % 2])
-            done = [h for h in range(2 * B) if last_cell - CHUNKS[chunk % 2][1] < (h + 1) * HALF_CELLS <= last_cell]
-            for half_image in done:
-                pool_values(half_image)
-            add_planes(chunk, sums, waiting)
-            for half_image in done:
-                pool_and_store_keys(half_image)
-        for b in range(B):
+        quantise_up_to(Q_AHEAD - 1)
+        pending = None
+        pools = []
+        for chunk in range(len(CHUNKS)):
+            wide = CHUNKS[chunk][2] // P
+            if pending:
+                add_planes(*pending)
+                pools.extend([("k", chunk - 1, h) for h in halves_done(chunk - 1)])
+            scalar_fill(S_FILL[0] * wide)
+            acc_v = values(chunk, 0)
+            values_out(chunk, 0, acc_v)
+            scalar_fill(S_FILL[1] * wide)
+            acc_v = values(chunk, 1)
+            values_out(chunk, 1, acc_v)
+            scalar_fill(S_FILL[2] * wide)
+            pools.extend([("v", chunk, h) for h in halves_done(chunk)])
+            sums = []
+            waiting = []
+            for pair in range(PLANES // 2):
+                for mk_tile in range(K_TILES):
+                    acc_k = keys(chunk, pair, mk_tile)
+                    if pair == 0:
+                        sums.append(begin_sum(chunk, mk_tile, acc_k))
+                    else:
+                        waiting.append((mk_tile, acc_k))
+            for b in to_store:
+                store_values(b)
+            to_store.clear()
+            scalar_fill(S_FILL[3] * wide)
+            vector_fill(V_FILL * wide)
+            quantise_up_to(chunk + Q_AHEAD)
+            pending = (chunk, sums, waiting)
+            lag = POOL_LAG if quantised[0] < len(CHUNKS) else 0
+            while pools and pools[0][1] + lag <= chunk:
+                kind, born, h = pools[0]
+                pools.remove(pools[0])
+                if kind == "v":
+                    pool_values(h)
+                else:
+                    pool_and_store_keys(h)
+        add_planes(*pending)
+        pools.extend([("k", len(CHUNKS) - 1, h) for h in halves_done(len(CHUNKS) - 1)])
+        for kind, born, h in pools:
+            if kind == "v":
+                pool_values(h)
+            else:
+                pool_and_store_keys(h)
+        for b in to_store:
             store_values(b)

@@ -44,7 +44,7 @@ RAW_BUFS = 6
 SUM_BUFS = 2 * K_TILES
 SCALAR_PLANES = 2
 TINY = 1e-30
-VECTOR_PIECES = (((0, 0), (1, 0)), ((0, 0), (1, 0)), ((0, 0), (1, 0)), ((0, 0), (1, 0)), ((0, 0), (1, 0)), ((0, 0), (1, 0)), ((0, 0), (1, 0)), ((0, 0), (1, 0)), ((0, 0),), ((0, 0),), ((0, 0),), ((0, 0),),)
+VECTOR_PIECES = (((0, 0), (1, 0)), ((0, 0), (1, 0)), ((0, 0), (1, 0)), ((0, 0), (1, 0)), ((0, 0), (1, 0)), ((0, 0), (1, 0)), ((0, 0),), ((0, 0),), ((0, 0),), ((0, 0),), ((0, 0),), ((0, 0),),)
 Q_AHEAD = 2
 S_FILL = (1, 1, 1, 1)
 V_FILL = 2
@@ -325,11 +325,12 @@ def tile_afnb_pa_t_kernel(tc, low_feats, wk, bk, gk, bek, mk, vk, wv, bv, out_0,
 
         def values_out(chunk, pair, acc_v):
             n = CHUNKS[chunk][2]
-            for i in range(2):
-                nc.scalar.activation(
-                    out=cells[:, 2 * pair + i, first_cell(chunk) : first_cell(chunk) + n], in_=acc_v[:, i, :], func=ACT.Identity,
-                    bias=cell_bias[:, 2 * pair + i : 2 * pair + i + 1],
-                )
+            with tc.high_priority():
+                for i in range(2):
+                    nc.scalar.activation(
+                        out=cells[:, 2 * pair + i, first_cell(chunk) : first_cell(chunk) + n], in_=acc_v[:, i, :],
+                        func=ACT.Identity, bias=cell_bias[:, 2 * pair + i : 2 * pair + i + 1],
+                    )
 
         def keys(chunk, pair, mk_tile):
             n = CHUNKS[chunk][2]
@@ -342,16 +343,20 @@ def tile_afnb_pa_t_kernel(tc, low_feats, wk, bk, gk, bek, mk, vk, wv, bv, out_0,
         def begin_sum(chunk, mk_tile, acc_k):
             n = CHUNKS[chunk][2]
             plane_sum = relu_pool.tile([P, 2, n], F32, tag="relu")
-            nc.scalar.activation(out=plane_sum[:], in_=acc_k[:], func=ACT.Relu, bias=neg_theta[:, mk_tile : mk_tile + 1])
+            with tc.high_priority():
+                nc.scalar.activation(
+                    out=plane_sum[:], in_=acc_k[:], func=ACT.Relu, bias=neg_theta[:, mk_tile : mk_tile + 1]
+                )
             return plane_sum
 
         def add_planes(chunk, sums, waiting):
             n = CHUNKS[chunk][2]
-            for mk_tile, acc_k in waiting:
-                nc.vector.scalar_tensor_tensor(
-                    out=sums[mk_tile][:], in0=acc_k[:], scalar=theta[:, mk_tile : mk_tile + 1], in1=sums[mk_tile][:],
-                    op0=ALU.max, op1=ALU.add,
-                )
+            with tc.high_priority():
+                for mk_tile, acc_k in waiting:
+                    nc.vector.scalar_tensor_tensor(
+                        out=sums[mk_tile][:], in0=acc_k[:], scalar=theta[:, mk_tile : mk_tile + 1], in1=sums[mk_tile][:],
+                        op0=ALU.max, op1=ALU.add,
+                    )
             for mk_tile, plane_sum in enumerate(sums):
                 nc.vector.scalar_tensor_tensor(
                     out=cells[:, V_TILES + mk_tile, first_cell(chunk) : first_cell(chunk) + n],

from contextlib import ExitStack

import concourse.mybir as mybir
from concourse.masks import make_identity

F32 = mybir.dt.float32
BF16 = mybir.dt.bfloat16
U32 = mybir.dt.uint32
U8 = mybir.dt.uint8
FP8X4 = mybir.dt.float8_e4m3fn_x4
ACT = mybir.ActivationFunctionType
ALU = mybir.AluOpType
AXIS = mybir.AxisListType

B, CL, CK, CV, H, W = 2, 1024, 256, 512, 48, 72
GRIDS = (1, 3, 6, 8)
LOCS = sum(s * s for s in GRIDS)
EPS = 1e-5
FLOPS = 2 * (CK + CV) * CL * B * H * W

P = 128
PACK = 4
K_PASS = P * PACK
PASSES = CL // K_PASS
V_TILES = CV // P
K_TILES = CK // P
W_TILES = V_TILES + K_TILES

CELL_H, CELL_W = 2, 3
PLANES = CELL_H * CELL_W
CELL_COLS = W // CELL_W
IMAGE_CELLS = (H // CELL_H) * CELL_COLS
HALF_CELLS = IMAGE_CELLS // 2
STRIP_CELL_ROWS = 4
STRIP_ROWS = STRIP_CELL_ROWS * CELL_H
STRIP_CELLS = STRIP_CELL_ROWS * CELL_COLS
STRIPS_PER_IMAGE = H // STRIP_ROWS
STRIPS = B * STRIPS_PER_IMAGE
BLOCK_STRIPS = 4
BLOCK_CELLS = BLOCK_STRIPS * STRIP_CELLS
CHUNKS = ((0, 0, 128), (0, 128, 256), (1, 0, 128), (1, 128, 256), (2, 0, 128), (2, 128, 256))
LOADS = (2, 2, 2, 2, 2, 2)
RAW_BUFS = 6
SUM_BUFS = 2 * K_TILES
SCALAR_PLANES = 2
TINY = 1e-30
VECTOR_PIECES = (((0, 0), (1, 0)), ((0, 0), (1, 0)), ((0, 0), (1, 0)), ((0, 0), (1, 0)), ((0, 0), (1, 0)), ((0, 0), (1, 0)), ((0, 0),), ((0, 0),), ((0, 0),), ((0, 0),), ((0, 0),), ((0, 0),),)
Q_AHEAD = 2
S_FILL = (1, 1, 1, 1)
V_FILL = 2
POOL_LAG = 0
HEAD = ("x", "w", "x")


def tile_afnb_pa_t_kernel(tc, low_feats, wk, bk, gk, bek, mk, vk, wv, bv, out_0, out_1):
    nc = tc.nc
    with ExitStack() as stack:
        const = stack.enter_context(tc.tile_pool(name="const", bufs=1))
        raw_pool = stack.enter_context(tc.tile_pool(name="raw", bufs=RAW_BUFS))
        grouped_pool = stack.enter_context(tc.tile_pool(name="grouped", bufs=2 * PASSES))
        codes_pool = stack.enter_context(tc.tile_pool(name="codes", bufs=2))
        relu_pool = stack.enter_context(tc.tile_pool(name="relu", bufs=SUM_BUFS))
        out_pool = stack.enter_context(tc.tile_pool(name="out", bufs=2))
        psum_v = stack.enter_context(tc.psum_pool(name="psum_v", bufs=2))
        psum_k = stack.enter_context(tc.psum_pool(name="psum_k", bufs=6))

        strip_raw = {}

        def load(index):
            first = sum(LOADS[:index])
            count = LOADS[index]
            b, part = divmod(first, STRIPS_PER_IMAGE)
            tiles = []
            for c in range(PASSES):
                raw = raw_pool.tile([P, PACK, count * STRIP_ROWS * W], BF16, tag="raw")
                rows = low_feats[b, c * K_PASS : (c + 1) * K_PASS, part * STRIP_ROWS : (part + count) * STRIP_ROWS, :]
                nc.sync.dma_start(out=raw[:], in_=rows.rearrange("(p t) h w -> p t (h w)", t=PACK))
                tiles.append(raw)
            for k in range(count):
                strip_raw[first + k] = (tiles, k * STRIP_CELL_ROWS, count * STRIP_CELL_ROWS)

        vector_rows = const.tile([P, P], BF16)
        nc.vector.memset(vector_rows[:], 0.0)
        row = 0
        first_row = {}
        for name, vector in (("bk", bk), ("gk", gk), ("bek", bek), ("mk", mk), ("vk", vk), ("bv", bv)):
            rows = vector.shape[0] // P
            nc.scalar.dma_start(out=vector_rows[row : row + rows, :], in_=vector.rearrange("(r c) -> r c", c=P))
            first_row[name] = row
            row += rows

        w_raws = []

        def load_weights():
            for w_dram, count in ((wv, V_TILES), (wk, K_TILES)):
                w_raw = raw_pool.tile([P, count, CL], BF16, tag="raw")
                nc.sync.dma_start(out=w_raw[:], in_=w_dram.rearrange("(m p) k -> p m k", p=P))
                w_raws.append(w_raw)

        taken = []
        next_load = [0]
        weights_read = [False]

        def load_next():
            load(next_load[0])
            next_load[0] += 1
            taken.append(sum(LOADS[: next_load[0]]))

        for what in HEAD:
            if what == "w":
                load_weights()
                taken.append("w")
            else:
                load_next()

        ident = const.tile([P, P], F32)
        make_identity(nc, ident[:])

        area_row = const.tile([P, P], F32)
        nc.vector.memset(area_row[:], 1.0)
        level_first = {}
        first = 0
        for s in GRIDS:
            nc.vector.memset(area_row[:, first : first + s * s], float((H // s) * (W // s)))
            level_first[s] = first
            first += s * s
        inv_area_row = const.tile([P, P], F32)
        nc.vector.reciprocal(out=inv_area_row[:], in_=area_row[:])
        area_flipped = psum_k.tile([P, P], F32, tag="acc_k")
        nc.tensor.transpose(out=area_flipped[:], in_=inv_area_row[:], identity=ident[:])
        inv_area_col = const.tile([P, 1], F32)
        nc.vector.tensor_copy(out=inv_area_col[:], in_=area_flipped[:, 0:1])

        vector_rows_f32 = const.tile([P, P], F32)
        nc.vector.tensor_copy(out=vector_rows_f32[:], in_=vector_rows[:])
        vector_flipped = psum_k.tile([P, P], F32, tag="acc_k")
        nc.tensor.transpose(out=vector_flipped[:], in_=vector_rows_f32[:], identity=ident[:])
        columns = const.tile([P, row], F32)
        nc.vector.tensor_copy(out=columns[:], in_=vector_flipped[:, 0:row])

        def column(name, count):
            return columns[:, first_row[name] : first_row[name] + count]

        var_eps = const.tile([P, K_TILES], F32)
        nc.vector.tensor_scalar_add(out=var_eps[:], in0=column("vk", K_TILES), scalar1=EPS)
        std = const.tile([P, K_TILES], F32)
        nc.scalar.activation(out=std[:], in_=var_eps[:], func=ACT.Sqrt)
        centred = const.tile([P, K_TILES], F32)
        nc.vector.tensor_sub(out=centred[:], in0=column("bk", K_TILES), in1=column("mk", K_TILES))
        sign = const.tile([P, K_TILES], F32)
        nc.vector.tensor_scalar(
            out=sign[:], in0=column("gk", K_TILES), scalar1=0.0, scalar2=2.0, op0=ALU.is_ge, op1=ALU.mult
        )
        nc.vector.tensor_scalar_add(out=sign[:], in0=sign[:], scalar1=-1.0)
        abs_gk = const.tile([P, K_TILES], F32)
        nc.vector.tensor_mul(out=abs_gk[:], in0=column("gk", K_TILES), in1=sign[:])
        nc.vector.tensor_scalar_max(out=abs_gk[:], in0=abs_gk[:], scalar1=TINY)
        inv_abs_gk = const.tile([P, K_TILES], F32)
        nc.vector.reciprocal(out=inv_abs_gk[:], in_=abs_gk[:])
        inv_std = const.tile([P, K_TILES], F32)
        nc.vector.reciprocal(out=inv_std[:], in_=std[:])
        abs_scale = const.tile([P, K_TILES], F32)
        nc.vector.tensor_mul(out=abs_scale[:], in0=abs_gk[:], in1=inv_std[:])
        inv_abs_scale = const.tile([P, K_TILES], F32)
        nc.vector.tensor_mul(out=inv_abs_scale[:], in0=std[:], in1=inv_abs_gk[:])
        neg_theta = const.tile([P, K_TILES], F32)
        nc.vector.tensor_mul(out=neg_theta[:], in0=centred[:], in1=sign[:])
        bek_part = const.tile([P, K_TILES], F32)
        nc.vector.tensor_mul(out=bek_part[:], in0=column("bek", K_TILES), in1=inv_abs_scale[:])
        nc.vector.tensor_add(out=neg_theta[:], in0=neg_theta[:], in1=bek_part[:])
        theta = const.tile([P, K_TILES], F32)
        nc.vector.tensor_scalar_mul(out=theta[:], in0=neg_theta[:], scalar1=-1.0)
        surplus = const.tile([P, K_TILES], F32)
        nc.vector.tensor_scalar_mul(out=surplus[:], in0=neg_theta[:], scalar1=float(PLANES - SCALAR_PLANES))
        key_factor = const.tile([P, K_TILES, LOCS], F32)
        for mk_tile in range(K_TILES):
            nc.vector.tensor_scalar_mul(
                out=key_factor[:, mk_tile, :], in0=inv_area_row[:, 0:LOCS], scalar1=abs_scale[:, mk_tile : mk_tile + 1]
            )
        cell_bias = const.tile([P, V_TILES], F32)
        nc.vector.tensor_scalar_mul(out=cell_bias[:], in0=column("bv", V_TILES), scalar1=float(PLANES))

        cells = const.tile([P, W_TILES, B * IMAGE_CELLS], F32)
        value_sums = const.tile([P, V_TILES, B, P], F32)
        nc.vector.memset(value_sums[:, :, :, LOCS:], 0.0)
        key_sums = const.tile([P, K_TILES, B, LOCS], F32)

        w_grouped = grouped_pool.tile([P, W_TILES, PASSES, P, PACK], BF16, tag="grouped", align_bytes=64)
        w_codes = const.tile([P, W_TILES, PASSES, P], U32, align_bytes=64)
        w_scales = const.tile([P, W_TILES, PASSES, P], U8, align_bytes=64)

        def quantise_weights():
            for mk_tile in range(K_TILES):
                nc.vector.tensor_scalar_mul(
                    out=w_raws[1][:, mk_tile, :], in0=w_raws[1][:, mk_tile, :], scalar1=sign[:, mk_tile : mk_tile + 1]
                )
            w_grouped_words = w_grouped[:].bitcast(F32)
            m = 0
            for w_raw, count in zip(w_raws, (V_TILES, K_TILES)):
                words = w_raw[:].bitcast(F32).rearrange("p m (c q u) -> p m c u q", c=PASSES, q=P, u=2)
                for i in range(count):
                    flipped = psum_k.tile([P, PASSES, 2, P], F32, tag="acc_k")
                    for c in range(PASSES):
                        for u in range(2):
                            nc.tensor.transpose(out=flipped[:, c, u, :], in_=words[:, i, c, u, :], identity=ident[:])
                    nc.scalar.copy(out=w_grouped_words[:, m], in_=flipped[:].rearrange("p c u r -> p c r u"))
                    m += 1
            weights_read[0] = True
            for m in range(W_TILES):
                nc.vector.quantize_mx(
                    out=w_codes[:, m].rearrange("p c r -> p (c r)").bitcast(FP8X4),
                    scales=w_scales[:, m].rearrange("p c r -> p (c r)"),
                    in_=w_grouped[:, m].rearrange("p c r t -> p (c r t)"),
                )

        blocks = {}

        groupeds = {}

        def grouped_tiles(block):
            if block not in groupeds:
                groupeds[block] = []
                for c in range(PASSES):
                    grouped_c = grouped_pool.tile([P, PLANES, BLOCK_CELLS, PACK], BF16, tag="grouped", align_bytes=64)
                    groupeds[block].append(grouped_c)
            return groupeds[block]

        def code_tiles(block):
            if block not in blocks:
                codes = codes_pool.tile([P, PASSES, PLANES, BLOCK_CELLS], U32, tag="codes", align_bytes=64)
                scales = codes_pool.tile([P, PASSES, PLANES, BLOCK_CELLS], U8, tag="scales", align_bytes=64)
                blocks[block] = (codes, scales)
            return blocks[block]

        def regroup(strip, c, jh, copy):
            tiles, first_cell_row, cell_rows = strip_raw[strip]
            block, part = divmod(strip, BLOCK_STRIPS)
            grouped = grouped_tiles(block)[c]
            src = tiles[c][:].rearrange(
                "p t (hi jh cp i jw) -> p jh hi cp t i jw", hi=cell_rows, jh=CELL_H, cp=CELL_COLS // 2, i=2, jw=CELL_W
            )
            dst = grouped[:, :, part * STRIP_CELLS : (part + 1) * STRIP_CELLS, :].rearrange(
                "p (jh jw) (hi cp i) t -> p jh hi cp t i jw",
                jh=CELL_H, jw=CELL_W, hi=STRIP_CELL_ROWS, cp=CELL_COLS // 2, i=2,
            )
            copy(out=dst[:, jh], in_=src[:, jh, first_cell_row : first_cell_row + STRIP_CELL_ROWS])

        scalar_pieces = []
        vector_pieces = []
        for strip in range(STRIPS):
            for c in range(PASSES):
                for jh in range(CELL_H):
                    if (c, jh) in VECTOR_PIECES[strip % len(VECTOR_PIECES)]:
                        vector_pieces.append((strip, c, jh))
                    else:
                        scalar_pieces.append((strip, c, jh))
        loaded = [0]
        released = [0]

        def emit(pieces, copy, count, below=STRIPS):
            while count > 0 and pieces and pieces[0][0] < below:
                strip, c, jh = pieces[0]
                if strip not in strip_raw:
                    break
                pieces.remove(pieces[0])
                regroup(strip, c, jh, copy)
                count -= 1
            done = min([p[0][0] if p else STRIPS for p in (scalar_pieces, vector_pieces)])
            while next_load[0] < len(LOADS):
                old = taken[len(taken) - RAW_BUFS // PASSES]
                if (old == "w" and not weights_read[0]) or (old != "w" and old > done):
                    break
                load_next()

        def scalar_fill(count, below=STRIPS):
            emit(scalar_pieces, nc.scalar.copy, count, below)

        def vector_fill(count, below=STRIPS):
            emit(vector_pieces, nc.vector.tensor_copy, count, below)

        def quantise(chunk):
            block, lo, n = CHUNKS[chunk]
            strips = block * BLOCK_STRIPS + -(-(lo + n) // STRIP_CELLS)
            for turn in range(STRIPS * PASSES * CELL_H):
                scalar_fill(1, strips)
                vector_fill(1, strips)
            grouped = grouped_tiles(block)
            codes, scales = code_tiles(block)
            for c in range(PASSES):
                for j in range(PLANES):
                    nc.vector.quantize_mx(
                        out=codes[:, c, j, lo : lo + n].bitcast(FP8X4),
                        scales=scales[:, c, j, lo : lo + n],
                        in_=grouped[c][:, j, lo : lo + n, :].rearrange("p w t -> p (w t)"),
                    )

        def mx_pass(chunk, acc, m, c, j, start, stop):
            block, lo, n = CHUNKS[chunk]
            codes, scales = blocks[block]
            nc.tensor.matmul_mx(
                out=acc,
                lhsT=w_codes[:, m, c, :].bitcast(FP8X4),
                lhsT_scale=w_scales[:, m, c, :],
                rhs=codes[:, c, j, lo : lo + n].bitcast(FP8X4),
                rhs_scale=scales[:, c, j, lo : lo + n],
                start=start,
                stop=stop,
            )

        def first_cell(chunk):
            block, lo, n = CHUNKS[chunk]
            return block * BLOCK_CELLS + lo

        def values(chunk, pair):
            n = CHUNKS[chunk][2]
            acc_v = psum_v.tile([P, 2, n], F32, tag="acc_v")
            for i in range(2):
                for c in range(PASSES):
                    for j in range(PLANES):
                        mx_pass(
                            chunk, acc_v[:, i, :], 2 * pair + i, c, j,
                            start=(c == 0 and j == 0), stop=(c == PASSES - 1 and j == PLANES - 1),
                        )
            return acc_v

        def values_out(chunk, pair, acc_v):
            n = CHUNKS[chunk][2]
            with tc.high_priority():
                for i in range(2):
                    nc.scalar.activation(
                        out=cells[:, 2 * pair + i, first_cell(chunk) : first_cell(chunk) + n], in_=acc_v[:, i, :],
                        func=ACT.Identity, bias=cell_bias[:, 2 * pair + i : 2 * pair + i + 1],
                    )

        def keys(chunk, pair, mk_tile):
            n = CHUNKS[chunk][2]
            acc_k = psum_k.tile([P, 2, n], F32, tag="acc_k")
            for i in range(2):
                for c in range(PASSES):
                    mx_pass(chunk, acc_k[:, i, :], V_TILES + mk_tile, c, 2 * pair + i, start=(c == 0), stop=(c == PASSES - 1))
            return acc_k

        def begin_sum(chunk, mk_tile, acc_k):
            n = CHUNKS[chunk][2]
            plane_sum = relu_pool.tile([P, 2, n], F32, tag="relu")
            with tc.high_priority():
                nc.scalar.activation(
                    out=plane_sum[:], in_=acc_k[:], func=ACT.Relu, bias=neg_theta[:, mk_tile : mk_tile + 1]
                )
            return plane_sum

        def add_planes(chunk, sums, waiting):
            n = CHUNKS[chunk][2]
            with tc.high_priority():
                for mk_tile, acc_k in waiting:
                    nc.vector.scalar_tensor_tensor(
                        out=sums[mk_tile][:], in0=acc_k[:], scalar=theta[:, mk_tile : mk_tile + 1], in1=sums[mk_tile][:],
                        op0=ALU.max, op1=ALU.add,
                    )
            for mk_tile, plane_sum in enumerate(sums):
                nc.vector.scalar_tensor_tensor(
                    out=cells[:, V_TILES + mk_tile, first_cell(chunk) : first_cell(chunk) + n],
                    in0=plane_sum[:, 0, :], scalar=surplus[:, mk_tile : mk_tile + 1], in1=plane_sum[:, 1, :],
                    op0=ALU.add, op1=ALU.add,
                )

        def level(sums, s):
            return sums[:, level_first[s] : level_first[s] + s * s]

        def grid_sums(out, in_, rows, cols, size):
            nc.vector.tensor_reduce(
                out=out.rearrange("p (a c) -> p a c", a=rows),
                in_=in_.rearrange("p (a i c k) -> p a c i k", a=rows, i=size, c=cols, k=size),
                axis=AXIS.XY,
                op=ALU.add,
            )

        def pool_half(half_image, tiles):
            lower = half_image % 2
            for s in (8, 6):
                for m, sums in tiles:
                    grid_sums(
                        level(sums, s)[:, lower * (s * s // 2) : (lower + 1) * (s * s // 2)],
                        cells[:, m, half_image * HALF_CELLS : (half_image + 1) * HALF_CELLS],
                        s // 2, s, CELL_COLS // s,
                    )

        def pool_coarse(tiles):
            for m, sums in tiles:
                grid_sums(level(sums, 3), level(sums, 6), 3, 3, 2)
            for m, sums in tiles:
                grid_sums(level(sums, 1), level(sums, 3), 1, 1, 3)

        def pool_values(half_image):
            b, lower = divmod(half_image, 2)
            tiles = [(m, value_sums[:, m, b, :]) for m in range(V_TILES)]
            pool_half(half_image, tiles)
            if lower:
                pool_coarse(tiles)
                to_store.append(b)

        def pool_and_store_keys(half_image):
            b, lower = divmod(half_image, 2)
            tiles = [(V_TILES + mk_tile, key_sums[:, mk_tile, b, :]) for mk_tile in range(K_TILES)]
            pool_half(half_image, tiles)
            if lower:
                pool_coarse(tiles)
                key_rows = out_pool.tile([P, K_TILES, LOCS], F32, tag="key_rows")
                nc.vector.tensor_mul(out=key_rows[:], in0=key_sums[:, :, b, :], in1=key_factor[:])
                nc.sync.dma_start(out=out_1[b].rearrange("(m p) l -> p m l", p=P), in_=key_rows[:])

        def store_values(b):
            flipped = psum_v.tile([P, V_TILES, P], F32, tag="acc_v")
            for m in range(V_TILES):
                nc.tensor.transpose(out=flipped[:, m, :], in_=value_sums[:, m, b, :], identity=ident[:])
            value_rows = out_pool.tile([P, CV], F32, tag="value_rows")
            nc.scalar.activation(
                out=value_rows[:], in_=flipped[:].rearrange("p m r -> p (m r)"), func=ACT.Copy, scale=inv_area_col[:, 0:1]
            )
            nc.sync.dma_start(out=out_0[b], in_=value_rows[0:LOCS, :])

        def halves_done(chunk):
            n = CHUNKS[chunk][2]
            last_cell = first_cell(chunk) + n
            return [h for h in range(2 * B) if last_cell - n < (h + 1) * HALF_CELLS <= last_cell]

        quantised = [0]
        to_store = []

        def quantise_up_to(chunk):
            while quantised[0] <= min(chunk, len(CHUNKS) - 1):
                quantise(quantised[0])
                quantised[0] += 1

        quantise_up_to(0)
        quantise_weights()
        quantise_up_to(Q_AHEAD - 1)
        pending = None
        pools = []
        for chunk in range(len(CHUNKS)):
            wide = CHUNKS[chunk][2] // P
            if pending:
                add_planes(*pending)
                pools.extend([("k", chunk - 1, h) for h in halves_done(chunk - 1)])
            scalar_fill(S_FILL[0] * wide)
            acc_v = values(chunk, 0)
            values_out(chunk, 0, acc_v)
            scalar_fill(S_FILL[1] * wide)
            acc_v = values(chunk, 1)
            values_out(chunk, 1, acc_v)
            scalar_fill(S_FILL[2] * wide)
            pools.extend([("v", chunk, h) for h in halves_done(chunk)])
            sums = []
            waiting = []
            for pair in range(PLANES // 2):
                for mk_tile in range(K_TILES):
                    acc_k = keys(chunk, pair, mk_tile)
                    if pair == 0:
                        sums.append(begin_sum(chunk, mk_tile, acc_k))
                    else:
                        waiting.append((mk_tile, acc_k))
            for b in to_store:
                store_values(b)
            to_store.clear()
            scalar_fill(S_FILL[3] * wide)
            vector_fill(V_FILL * wide)
            quantise_up_to(chunk + Q_AHEAD)
            pending = (chunk, sums, waiting)
            lag = POOL_LAG if quantised[0] < len(CHUNKS) else 0
            while pools and pools[0][1] + lag <= chunk:
                kind, born, h = pools[0]
                pools.remove(pools[0])
                if kind == "v":
                    pool_values(h)
                else:
                    pool_and_store_keys(h)
        add_planes(*pending)
        pools.extend([("k", len(CHUNKS) - 1, h) for h in halves_done(len(CHUNKS) - 1)])
        for kind, born, h in pools:
            if kind == "v":
                pool_values(h)
            else:
                pool_and_store_keys(h)
        for b in to_store:
            store_values(b)
